import numpy as np
import ml_dtypes


def mxq(x, axis, fmt="e4m3"):
    dtype, down = {"e4m3": (ml_dtypes.float8_e4m3fn, 7), "e5m2": (ml_dtypes.float8_e5m2, 14)}[fmt]
    v = np.moveaxis(np.asarray(x, np.float32).astype(ml_dtypes.bfloat16).astype(np.float64), axis, -1)
    blocks = v.reshape(v.shape[:-1] + (-1, 32))
    amax = np.abs(blocks).max(-1, keepdims=True)
    byte = np.maximum(np.where(amax > 0, np.frexp(amax)[1] - 1 + 127, 0) - down, 1)
    scale = np.exp2(byte - 127.0)
    codes = (blocks / scale).astype(np.float32).astype(dtype).astype(np.float64)
    return np.moveaxis((codes * scale).reshape(v.shape), -1, axis)


WIDE = False


def mx_kscale(k):
    if not WIDE:
        return np.ones(k)
    levels = np.array([10, -10, 5, -5, 0])
    a = np.random.permutation(np.resize(levels, k // 512 * 4)).reshape(k // 512, 4)
    idx = np.arange(k)
    return np.exp2(a[idx // 512, idx % 128 // 32])


BF16 = ml_dtypes.bfloat16


def bf(x):
    return np.asarray(x, np.float32).astype(BF16)


def f64(x):
    return np.asarray(x).astype(np.float64)


B, L, D_G, D_SP, H, OUT = 2, 64, 512, 512, 512, 640


def softmax1(m):
    e = np.exp(m - m.max())
    return e / e.sum()


def setup_inputs():
    s, u = mx_kscale(D_G), mx_kscale(D_SP)
    s2, u2 = np.concatenate([s, s])[:, None], np.concatenate([u, u])[:, None]
    mix0 = np.array([0.4, -0.4])
    return {
        "global_outputs": bf(np.random.standard_normal((B, L, D_G)) * s),
        "sp_outputs": bf(np.random.standard_normal((B, L, D_SP)) * u),
        "W_utt": bf(np.random.standard_normal((D_G + D_G, H)) * 0.5 / np.sqrt(D_G) / s2),
        "b_utt": bf(np.random.standard_normal(H) * 0.3),
        "W_sp": bf(np.random.standard_normal((D_SP + D_SP, H)) * 0.5 / np.sqrt(D_SP) / u2),
        "b_sp": bf(np.random.standard_normal(H) * 0.3),
        "W2": bf(np.random.standard_normal((H, OUT)) * 1.5 / np.sqrt(H)),
        "b2": bf(np.random.standard_normal(OUT) * 0.3),
        "mix_w": bf(mix0 + 0.1 * np.random.standard_normal(mix0.shape)),
        "gamma": bf(np.atleast_1d(1.5 + 0.1 * np.random.standard_normal())),
    }


def reference(global_outputs, sp_outputs, W_utt, b_utt, W_sp, b_sp, W2, b2, mix_w, gamma):
    gq = mxq(f64(global_outputs), 2, "e4m3")
    wu = f64(W_utt)
    g_j = gq @ mxq(wu[:D_G], 0, "e4m3")
    g_i = gq @ mxq(wu[D_G:], 0, "e4m3")
    utt_hidden = np.tanh(g_j[:, None, :, :] + g_i[:, :, None, :] + f64(b_utt))

    sq = mxq(f64(sp_outputs), 2, "e4m3")
    ws = f64(W_sp)
    s_j = sq @ mxq(ws[:D_SP], 0, "e4m3")
    s_i = sq @ mxq(ws[D_SP:], 0, "e4m3")
    sp_hidden = np.tanh(s_j[:, None, :, :] + s_i[:, :, None, :] + f64(b_sp))

    w = softmax1(f64(mix_w))
    state_hidden = f64(gamma) * (w[0] * utt_hidden + w[1] * sp_hidden)

    return np.tanh((mxq(state_hidden, 3, "e4m3") @ mxq(f64(W2), 0, "e4m3")) + f64(b2))

@@ -1,0 +1,243 @@
+from contextlib import ExitStack
+
+import concourse.mybir as mybir
+from concourse.masks import make_identity
+
+F32 = mybir.dt.float32
+BF16 = mybir.dt.bfloat16
+I32 = mybir.dt.int32
+U32 = mybir.dt.uint32
+U8 = mybir.dt.uint8
+FP8X4 = mybir.dt.float8_e4m3fn_x4
+ACT = mybir.ActivationFunctionType
+ALU = mybir.AluOpType
+
+P = 128
+B, L, D, H, OUT = 2, 64, 512, 512, 640
+IB = 8
+NT = B * (L // IB)
+FLOPS = 4 * 2 * (B * L) * D * H + 2 * (B * L * L) * H * OUT
+PINNED = False
+
+
+def tile_stateencoder_pa_kernel(
+    tc, global_outputs, sp_outputs, W_utt, b_utt, W_sp, b_sp, W2, b2, mix_w, gamma, out
+):
+    nc = tc.nc
+    out_rows = out.rearrange("b i j o -> (b i j) o")
+    with ExitStack() as ctx:
+        keep = ctx.enter_context(tc.tile_pool(name="keep", bufs=1))
+        rot = ctx.enter_context(tc.tile_pool(name="rot", bufs=2))
+        psum = ctx.enter_context(tc.psum_pool(name="psum", bufs=1))
+        if PINNED:
+            ctx.enter_context(tc.manual_schedule())
+
+        x_in = [global_outputs, sp_outputs]
+        w_in = [W_utt, W_sp]
+        x_sb = [keep.tile([P, D], BF16, name="x_sb%d" % s) for s in range(2)]
+        w_raw = [keep.tile([P, 8, H], BF16, name="w_raw%d" % s) for s in range(2)]
+        w2_raw = keep.tile([P, 4, OUT], BF16, name="w2_raw")
+        bt = keep.tile([P, P], BF16, name="bt")
+        b2b = keep.tile([P, OUT], BF16, name="b2b")
+        mw = keep.tile([P, 2], BF16, name="mw")
+        gm = keep.tile([P, 1], BF16, name="gm")
+        ident = keep.tile([P, P], BF16, name="ident")
+
+        nc.gpsimd.memset(bt, 0.0)
+        make_identity(nc, ident)
+        with nc.allow_non_contiguous_dma(reason="small vectors"):
+            nc.scalar.dma_start(out=bt[0:4, :], in_=b_utt.rearrange("(t p) -> t p", p=P))
+            nc.scalar.dma_start(out=bt[4:8, :], in_=b_sp.rearrange("(t p) -> t p", p=P))
+            nc.scalar.dma_start(out=mw, in_=mix_w.partition_broadcast(P))
+            nc.scalar.dma_start(out=gm, in_=gamma.partition_broadcast(P))
+        for s in range(2):
+            nc.sync.dma_start(out=x_sb[s], in_=x_in[s].rearrange("b l d -> (b l) d"))
+            nc.sync.dma_start(out=w_raw[s], in_=w_in[s].rearrange("(s p) n -> p s n", p=P))
+        nc.sync.dma_start(out=w2_raw, in_=W2.rearrange("(k p) n -> p k n", p=P))
+        nc.scalar.dma_start(out=b2b, in_=b2.partition_broadcast(P))
+
+        x1 = [keep.tile([P, P, 4], BF16, name="x1_%d" % s, align_bytes=64) for s in range(2)]
+        x4 = [keep.tile([P, P, 4, 4], BF16, name="x4_%d" % s, align_bytes=64) for s in range(2)]
+        xc1 = keep.tile([P, 2, P], U32, name="xc1", align_bytes=64)
+        xs1 = keep.tile([P, 2, P], U8, name="xs1", align_bytes=64)
+        xc4 = keep.tile([P, 2, 4 * P], U32, name="xc4", align_bytes=64)
+        xs4 = keep.tile([P, 2, 4 * P], U8, name="xs4", align_bytes=64)
+        a_c = keep.tile([P, 2, 1024], U32, name="a_c", align_bytes=64)
+        a_s = keep.tile([P, 2, 1024], U8, name="a_s", align_bytes=64)
+        wc = keep.tile([P, 2, 4, 256], U32, name="wc", align_bytes=64)
+        ws = keep.tile([P, 2, 4, 256], U8, name="ws", align_bytes=64)
+        w2g = keep.tile([P, OUT, 4], BF16, name="w2g", align_bytes=64)
+        w2c = keep.tile([P, OUT], U32, name="w2c", align_bytes=64)
+        w2s = keep.tile([P, OUT], U8, name="w2s", align_bytes=64)
+        bias_sb = keep.tile([P, 8], F32, name="bias_sb")
+        dd = keep.tile([P, 1], F32, name="dd")
+        rr = keep.tile([P, 1], F32, name="rr")
+        den = keep.tile([P, 1], F32, name="den")
+        w1 = keep.tile([P, 1], F32, name="w1")
+        c1 = keep.tile([P, 1], F32, name="c1")
+
+        nc.vector.memset(xs1.rearrange("p s c -> p (s c)").bitcast(I32), 0)
+        nc.vector.memset(xs4.rearrange("p s c -> p (s c)").bitcast(I32), 0)
+
+        nc.vector.tensor_tensor(out=dd, in0=mw[:, 0:1], in1=mw[:, 1:2], op=ALU.subtract)
+        nc.vector.tensor_scalar(out=dd, in0=dd, scalar1=30.0, scalar2=-30.0, op0=ALU.min, op1=ALU.max)
+        nc.scalar.activation(out=rr, in_=dd, func=ACT.Exp)
+        nc.vector.tensor_scalar(out=den, in0=rr, scalar1=1.0, scalar2=None, op0=ALU.add)
+        nc.vector.reciprocal(out=w1, in_=den)
+        nc.vector.tensor_tensor(out=c1, in0=w1, in1=gm, op=ALU.mult)
+
+        btp = psum.tile([P, P], BF16, name="btp", tag="pre", bufs=3)
+        nc.tensor.transpose(btp, bt, ident)
+        nc.vector.tensor_copy(out=bias_sb, in_=btp[:, 0:8])
+
+        def prep_x(s):
+            xt = psum.tile([P, 4, P], BF16, name="xt", tag="pre", bufs=3)
+            for t in range(4):
+                nc.tensor.transpose(xt[:, t, :], x_sb[s][:, P * t : P * (t + 1)], ident)
+            nc.vector.tensor_copy(out=x1[s], in_=xt.rearrange("p t r -> p r t"))
+            nc.vector.tensor_copy(out=x4[s], in_=x1[s].unsqueeze(2).to_broadcast([P, P, 4, 4]))
+            nc.vector.quantize_mx(
+                out=xc1[:, s, :].bitcast(FP8X4), scales=xs1[:, s, :],
+                in_=x1[s].rearrange("p r t -> p (r t)"),
+            )
+            nc.vector.quantize_mx(
+                out=xc4[:, s, :].bitcast(FP8X4), scales=xs4[:, s, :],
+                in_=x4[s].rearrange("p r c t -> p (r c t)"),
+            )
+            nc.vector.tensor_copy(
+                out=a_c[:, s, :].bitcast(I32).rearrange("p (b r j) -> p b r j", b=2, r=IB),
+                in_=xc1[:, s, :].bitcast(I32).rearrange("p (b j) -> p b j", b=2)
+                .unsqueeze(2).to_broadcast([P, 2, IB, L]),
+            )
+            nc.vector.tensor_copy(
+                out=a_s[:, s, :].bitcast(I32).rearrange("p (b r w) -> p b r w", b=2, r=IB),
+                in_=xs1[:, s, :].bitcast(I32).rearrange("p (b w) -> p b w", b=2)
+                .unsqueeze(2).to_broadcast([P, 2, IB, L // 4]),
+            )
+
+        def prep_w(s, c):
+            wg = rot.tile([P, 2, P, 4], BF16, name="wg", tag="wg", bufs=3, align_bytes=64)
+            nc.vector.tensor_copy(
+                out=wg, in_=w_raw[s][:, :, P * c : P * (c + 1)].rearrange("p (g k) m -> p g m k", g=2)
+            )
+            nc.vector.quantize_mx(
+                out=wc[:, s, c, :].bitcast(FP8X4), scales=ws[:, s, c, :],
+                in_=wg.rearrange("p g m k -> p (g m k)"),
+            )
+
+        def prep_w2():
+            nc.gpsimd.tensor_scalar(
+                out=w2g, in0=w2_raw.rearrange("p k n -> p n k"), scalar1=1.0, scalar2=0.0,
+                op0=ALU.mult, op1=ALU.add,
+            )
+            flat = w2g.rearrange("p n k -> p (n k)")
+            nc.vector.quantize_mx(out=w2c[:, 0:512].bitcast(FP8X4), scales=w2s[:, 0:512], in_=flat[:, 0:2048])
+            nc.vector.quantize_mx(out=w2c[:, 512:640].bitcast(FP8X4), scales=w2s[:, 512:640], in_=flat[:, 2048:2560])
+
+        live = {}
+
+        def build_b(n, streams):
+            tok0 = IB * n
+            if ("b", n) not in live:
+                b_c = rot.tile([P, 2, 512], U32, name="b_c", tag="b_c", bufs=3, align_bytes=64)
+                b_s = rot.tile([P, 2, 512], U8, name="b_s", tag="b_s", bufs=3, align_bytes=64)
+                live[("b", n)] = (b_c, b_s)
+            b_c, b_s = live[("b", n)]
+            for s in streams:
+                nc.vector.tensor_copy(
+                    out=b_c[:, s, :].bitcast(I32).rearrange("p (i j) -> p i j", i=IB),
+                    in_=xc1[:, s, tok0 : tok0 + IB].bitcast(I32).unsqueeze(2).to_broadcast([P, IB, L]),
+                )
+                nc.vector.tensor_copy(
+                    out=b_s[:, s, :].bitcast(I32).rearrange("p (i w) -> p i w", i=IB),
+                    in_=xs4[:, s, 4 * tok0 : 4 * (tok0 + IB)].bitcast(I32)
+                    .unsqueeze(2).to_broadcast([P, IB, L // 4]),
+                )
+
+        def hidden(n):
+            b = n // (L // IB)
+            b_c, b_s = live[("b", n)]
+            acts = []
+            for s in range(2):
+                hs = rot.tile([P, 4, 512], F32, name="hs%d" % s, tag="hs%d" % s, bufs=3)
+                acts.append(hs)
+                for t in range(4):
+                    pre = psum.tile([P, 512], F32, name="pre", tag="pre", bufs=3)
+                    nc.tensor.matmul_mx(
+                        out=pre,
+                        lhsT=wc[:, s, t, 0:P].bitcast(FP8X4), lhsT_scale=ws[:, s, t, 0:P],
+                        rhs=a_c[:, s, 512 * b : 512 * (b + 1)].bitcast(FP8X4),
+                        rhs_scale=a_s[:, s, 512 * b : 512 * (b + 1)],
+                        start=True, stop=False,
+                    )
+                    nc.tensor.matmul_mx(
+                        out=pre,
+                        lhsT=wc[:, s, t, P : 2 * P].bitcast(FP8X4), lhsT_scale=ws[:, s, t, P : 2 * P],
+                        rhs=b_c[:, s, :].bitcast(FP8X4), rhs_scale=b_s[:, s, :],
+                        start=False, stop=True,
+                    )
+                    nc.scalar.activation(
+                        out=hs[:, t, :], in_=pre, func=ACT.Tanh,
+                        bias=bias_sb[:, 4 * s + t : 4 * s + t + 1], scale=1.0,
+                    )
+            live[("h", n)] = acts
+
+        def mix(n):
+            hu, hp = live[("h", n)]
+            nc.vector.scalar_tensor_tensor(
+                out=hp.rearrange("p t w -> p (t w)"), in0=hu.rearrange("p t w -> p (t w)"),
+                scalar=rr[:, 0:1], in1=hp.rearrange("p t w -> p (t w)"), op0=ALU.mult, op1=ALU.add,
+            )
+            st = rot.tile([P, 512, 4], BF16, name="st", tag="st", bufs=2, align_bytes=64)
+            nc.vector.tensor_scalar(
+                out=st, in0=hp.rearrange("p t w -> p w t"), scalar1=c1[:, 0:1], scalar2=None, op0=ALU.mult
+            )
+            s_c = rot.tile([P, 512], U32, name="s_c", tag="s_c", bufs=2, align_bytes=64)
+            s_s = rot.tile([P, 512], U8, name="s_s", tag="s_s", bufs=2, align_bytes=64)
+            nc.vector.quantize_mx(out=s_c.bitcast(FP8X4), scales=s_s, in_=st.rearrange("p w t -> p (w t)"))
+            zs = rot.tile([P, 4, OUT], F32, name="zs", tag="zs", bufs=3)
+            z1 = psum.tile([P, 4, P], F32, name="z1", tag="z1", bufs=1)
+            for r in range(4):
+                z5 = psum.tile([P, 512], F32, name="z5", tag="z5", bufs=4)
+                cols = slice(P * r, P * (r + 1))
+                nc.tensor.matmul_mx(
+                    out=z5, lhsT=s_c[:, cols].bitcast(FP8X4), lhsT_scale=s_s[:, cols],
+                    rhs=w2c[:, 0:512].bitcast(FP8X4), rhs_scale=w2s[:, 0:512], start=True, stop=True,
+                )
+                nc.tensor.matmul_mx(
+                    out=z1[:, r, :], lhsT=s_c[:, cols].bitcast(FP8X4), lhsT_scale=s_s[:, cols],
+                    rhs=w2c[:, 512:640].bitcast(FP8X4), rhs_scale=w2s[:, 512:640], start=True, stop=True,
+                )
+                nc.vector.tensor_tensor(out=zs[:, r, 0:512], in0=z5, in1=b2b[:, 0:512], op=ALU.add)
+            nc.vector.tensor_tensor(
+                out=zs[:, :, 512:640], in0=z1,
+                in1=b2b[:, 512:640].unsqueeze(1).to_broadcast([P, 4, P]), op=ALU.add,
+            )
+            live[("z", n)] = zs
+
+        def finish(n):
+            zs = live[("z", n)]
+            for r in range(4):
+                nc.scalar.activation(out=zs[:, r, :], in_=zs[:, r, :], func=ACT.Tanh)
+                row0 = 512 * n + P * r
+                nc.sync.dma_start(out=out_rows[row0 : row0 + P, :], in_=zs[:, r, :])
+
+        prep_x(0)
+        prep_w(0, 0)
+        build_b(0, [0])
+        for c in range(1, 4):
+            prep_w(0, c)
+        prep_x(1)
+        build_b(0, [1])
+        for c in range(4):
+            prep_w(1, c)
+        prep_w2()
+        for n in range(NT + 2):
+            if n + 1 < NT:
+                build_b(n + 1, [0, 1])
+            if n < NT:
+                hidden(n)
+            if 0 <= n - 1 < NT:
+                mix(n - 1)
+            if 0 <= n - 2 < NT:
+                finish(n - 2)

@@ -17,7 +17,12 @@ B, L, D, H, OUT = 2, 64, 512, 512, 640
 IB = 8
 NT = B * (L // IB)
 FLOPS = 4 * 2 * (B * L) * D * H + 2 * (B * L * L) * H * OUT
-PINNED = False
+PINNED = True
+TS_ENGINE = "G"
+LAG = 3
+Z_POS = 3
+FINAL_SLOTS = (2, 4, 6, 7)
+STT_PIECES = ((0, 2), (2, 3), (3, 4))
 
 
 def tile_stateencoder_pa_kernel(
@@ -42,8 +47,11 @@ def tile_stateencoder_pa_kernel(
         mw = keep.tile([P, 2], BF16, name="mw")
         gm = keep.tile([P, 1], BF16, name="gm")
         ident = keep.tile([P, P], BF16, name="ident")
+        zero1 = keep.tile([P, 1], F32, name="zero1")
+        one1 = keep.tile([P, 1], F32, name="one1")
 
         nc.gpsimd.memset(bt, 0.0)
+        nc.gpsimd.memset(zero1, 0.0)
         make_identity(nc, ident)
         with nc.allow_non_contiguous_dma(reason="small vectors"):
             nc.scalar.dma_start(out=bt[0:4, :], in_=b_utt.rearrange("(t p) -> t p", p=P))
@@ -52,9 +60,14 @@ def tile_stateencoder_pa_kernel(
             nc.scalar.dma_start(out=gm, in_=gamma.partition_broadcast(P))
         for s in range(2):
             nc.sync.dma_start(out=x_sb[s], in_=x_in[s].rearrange("b l d -> (b l) d"))
-            nc.sync.dma_start(out=w_raw[s], in_=w_in[s].rearrange("(s p) n -> p s n", p=P))
+        for s in range(2):
+            w_view = w_in[s].rearrange("(s p) n -> p s n", p=P)
+            for half in range(2):
+                cols = slice(256 * half, 256 * (half + 1))
+                nc.sync.dma_start(out=w_raw[s][:, :, cols], in_=w_view[:, :, cols])
         nc.sync.dma_start(out=w2_raw, in_=W2.rearrange("(k p) n -> p k n", p=P))
         nc.scalar.dma_start(out=b2b, in_=b2.partition_broadcast(P))
+        nc.scalar.activation(out=one1, in_=zero1, func=ACT.Exp)
 
         x1 = [keep.tile([P, P, 4], BF16, name="x1_%d" % s, align_bytes=64) for s in range(2)]
         x4 = [keep.tile([P, P, 4, 4], BF16, name="x4_%d" % s, align_bytes=64) for s in range(2)]
@@ -75,130 +88,146 @@ def tile_stateencoder_pa_kernel(
         den = keep.tile([P, 1], F32, name="den")
         w1 = keep.tile([P, 1], F32, name="w1")
         c1 = keep.tile([P, 1], F32, name="c1")
+        xs4_words = xs4.rearrange("p s c -> p (s c)").bitcast(I32).rearrange("p (s k) -> p s k", s=2)
 
         nc.vector.memset(xs1.rearrange("p s c -> p (s c)").bitcast(I32), 0)
         nc.vector.memset(xs4.rearrange("p s c -> p (s c)").bitcast(I32), 0)
 
-        nc.vector.tensor_tensor(out=dd, in0=mw[:, 0:1], in1=mw[:, 1:2], op=ALU.subtract)
-        nc.vector.tensor_scalar(out=dd, in0=dd, scalar1=30.0, scalar2=-30.0, op0=ALU.min, op1=ALU.max)
-        nc.scalar.activation(out=rr, in_=dd, func=ACT.Exp)
-        nc.vector.tensor_scalar(out=den, in0=rr, scalar1=1.0, scalar2=None, op0=ALU.add)
-        nc.vector.reciprocal(out=w1, in_=den)
-        nc.vector.tensor_tensor(out=c1, in0=w1, in1=gm, op=ALU.mult)
+        def quant_x4(s, tok0, tok1):
+            nc.vector.quantize_mx(
+                out=xc4[:, s, 4 * tok0 : 4 * tok1].bitcast(FP8X4), scales=xs4[:, s, 4 * tok0 : 4 * tok1],
+                in_=x4[s][:, tok0:tok1].rearrange("p r c t -> p (r c t)"),
+            )
 
-        btp = psum.tile([P, P], BF16, name="btp", tag="pre", bufs=3)
-        nc.tensor.transpose(btp, bt, ident)
-        nc.vector.tensor_copy(out=bias_sb, in_=btp[:, 0:8])
+        def copy_x4(s, tok0, tok1):
+            nc.vector.tensor_copy(
+                out=x4[s][:, tok0:tok1],
+                in_=x1[s][:, tok0:tok1].unsqueeze(2).to_broadcast([P, tok1 - tok0, 4, 4]),
+            )
 
-        def prep_x(s):
+        def build_a(s, b):
+            nc.vector.tensor_copy(
+                out=a_c[:, s, 512 * b : 512 * (b + 1)].bitcast(I32).rearrange("p (r j) -> p r j", r=IB),
+                in_=xc1[:, s, L * b : L * (b + 1)].bitcast(I32).unsqueeze(1).to_broadcast([P, IB, L]),
+            )
+            nc.vector.tensor_copy(
+                out=a_s[:, s, 512 * b : 512 * (b + 1)].bitcast(I32).rearrange("p (r w) -> p r w", r=IB),
+                in_=xs1[:, s, L * b : L * (b + 1)].bitcast(I32).unsqueeze(1).to_broadcast([P, IB, L // 4]),
+            )
+
+        def x_chain(s):
             xt = psum.tile([P, 4, P], BF16, name="xt", tag="pre", bufs=3)
             for t in range(4):
                 nc.tensor.transpose(xt[:, t, :], x_sb[s][:, P * t : P * (t + 1)], ident)
             nc.vector.tensor_copy(out=x1[s], in_=xt.rearrange("p t r -> p r t"))
-            nc.vector.tensor_copy(out=x4[s], in_=x1[s].unsqueeze(2).to_broadcast([P, P, 4, 4]))
             nc.vector.quantize_mx(
                 out=xc1[:, s, :].bitcast(FP8X4), scales=xs1[:, s, :],
                 in_=x1[s].rearrange("p r t -> p (r t)"),
             )
-            nc.vector.quantize_mx(
-                out=xc4[:, s, :].bitcast(FP8X4), scales=xs4[:, s, :],
-                in_=x4[s].rearrange("p r c t -> p (r c t)"),
-            )
-            nc.vector.tensor_copy(
-                out=a_c[:, s, :].bitcast(I32).rearrange("p (b r j) -> p b r j", b=2, r=IB),
-                in_=xc1[:, s, :].bitcast(I32).rearrange("p (b j) -> p b j", b=2)
-                .unsqueeze(2).to_broadcast([P, 2, IB, L]),
-            )
-            nc.vector.tensor_copy(
-                out=a_s[:, s, :].bitcast(I32).rearrange("p (b r w) -> p b r w", b=2, r=IB),
-                in_=xs1[:, s, :].bitcast(I32).rearrange("p (b w) -> p b w", b=2)
-                .unsqueeze(2).to_broadcast([P, 2, IB, L // 4]),
-            )
+            copy_x4(s, 0, 32)
+            quant_x4(s, 0, 32)
+            build_a(s, 0)
 
-        def prep_w(s, c):
-            wg = rot.tile([P, 2, P, 4], BF16, name="wg", tag="wg", bufs=3, align_bytes=64)
-            nc.vector.tensor_copy(
-                out=wg, in_=w_raw[s][:, :, P * c : P * (c + 1)].rearrange("p (g k) m -> p g m k", g=2)
-            )
+        def x_rest(s):
+            copy_x4(s, 32, 128)
+            quant_x4(s, 32, 64)
+            quant_x4(s, 64, 128)
+            build_a(s, 1)
+
+        w_grouped = {}
+
+        def regroup_w(s, c, engine):
+            wg = rot.tile([P, 2, P, 4], BF16, name="wg", tag="wg", bufs=4, align_bytes=64)
+            src = w_raw[s][:, :, P * c : P * (c + 1)].rearrange("p (g k) m -> p g m k", g=2)
+            if engine == "V":
+                nc.vector.tensor_copy(out=wg, in_=src)
+            elif engine == "S":
+                nc.scalar.copy(out=wg, in_=src)
+            else:
+                nc.gpsimd.tensor_scalar(out=wg, in0=src, scalar1=1.0, scalar2=0.0, op0=ALU.mult, op1=ALU.add)
+            w_grouped[(s, c)] = wg
+
+        def quant_w(s, c):
             nc.vector.quantize_mx(
                 out=wc[:, s, c, :].bitcast(FP8X4), scales=ws[:, s, c, :],
-                in_=wg.rearrange("p g m k -> p (g m k)"),
+                in_=w_grouped[(s, c)].rearrange("p g m k -> p (g m k)"),
             )
-
-        def prep_w2():
-            nc.gpsimd.tensor_scalar(
-                out=w2g, in0=w2_raw.rearrange("p k n -> p n k"), scalar1=1.0, scalar2=0.0,
-                op0=ALU.mult, op1=ALU.add,
-            )
-            flat = w2g.rearrange("p n k -> p (n k)")
-            nc.vector.quantize_mx(out=w2c[:, 0:512].bitcast(FP8X4), scales=w2s[:, 0:512], in_=flat[:, 0:2048])
-            nc.vector.quantize_mx(out=w2c[:, 512:640].bitcast(FP8X4), scales=w2s[:, 512:640], in_=flat[:, 2048:2560])
 
         live = {}
 
         def build_b(n, streams):
             tok0 = IB * n
             if ("b", n) not in live:
-                b_c = rot.tile([P, 2, 512], U32, name="b_c", tag="b_c", bufs=3, align_bytes=64)
-                b_s = rot.tile([P, 2, 512], U8, name="b_s", tag="b_s", bufs=3, align_bytes=64)
+                b_c = rot.tile([P, 2, 512], U32, name="b_c", tag="b_c", bufs=2, align_bytes=64)
+                b_s = rot.tile([P, 2, 512], U8, name="b_s", tag="b_s", bufs=2, align_bytes=64)
                 live[("b", n)] = (b_c, b_s)
             b_c, b_s = live[("b", n)]
-            for s in streams:
-                nc.vector.tensor_copy(
-                    out=b_c[:, s, :].bitcast(I32).rearrange("p (i j) -> p i j", i=IB),
-                    in_=xc1[:, s, tok0 : tok0 + IB].bitcast(I32).unsqueeze(2).to_broadcast([P, IB, L]),
-                )
-                nc.vector.tensor_copy(
-                    out=b_s[:, s, :].bitcast(I32).rearrange("p (i w) -> p i w", i=IB),
-                    in_=xs4[:, s, 4 * tok0 : 4 * (tok0 + IB)].bitcast(I32)
-                    .unsqueeze(2).to_broadcast([P, IB, L // 4]),
-                )
+            s0, s1 = streams[0], streams[-1] + 1
+            ns = s1 - s0
+            nc.vector.tensor_copy(
+                out=b_c[:, s0:s1, :].bitcast(I32).rearrange("p s (i j) -> p s i j", i=IB),
+                in_=xc1[:, s0:s1, tok0 : tok0 + IB].bitcast(I32).unsqueeze(3).to_broadcast([P, ns, IB, L]),
+            )
+            nc.vector.tensor_copy(
+                out=b_s.rearrange("p s c -> p (s c)").bitcast(I32)
+                .rearrange("p (s i w) -> p s i w", s=2, i=IB)[:, s0:s1],
+                in_=xs4_words[:, s0:s1, tok0 : tok0 + IB].unsqueeze(3).to_broadcast([P, ns, IB, L // 4]),
+            )
 
-        def hidden(n):
+        def pre_act(n, s, t):
             b = n // (L // IB)
             b_c, b_s = live[("b", n)]
-            acts = []
-            for s in range(2):
-                hs = rot.tile([P, 4, 512], F32, name="hs%d" % s, tag="hs%d" % s, bufs=3)
-                acts.append(hs)
-                for t in range(4):
-                    pre = psum.tile([P, 512], F32, name="pre", tag="pre", bufs=3)
-                    nc.tensor.matmul_mx(
-                        out=pre,
-                        lhsT=wc[:, s, t, 0:P].bitcast(FP8X4), lhsT_scale=ws[:, s, t, 0:P],
-                        rhs=a_c[:, s, 512 * b : 512 * (b + 1)].bitcast(FP8X4),
-                        rhs_scale=a_s[:, s, 512 * b : 512 * (b + 1)],
-                        start=True, stop=False,
-                    )
-                    nc.tensor.matmul_mx(
-                        out=pre,
-                        lhsT=wc[:, s, t, P : 2 * P].bitcast(FP8X4), lhsT_scale=ws[:, s, t, P : 2 * P],
-                        rhs=b_c[:, s, :].bitcast(FP8X4), rhs_scale=b_s[:, s, :],
-                        start=False, stop=True,
-                    )
-                    nc.scalar.activation(
-                        out=hs[:, t, :], in_=pre, func=ACT.Tanh,
-                        bias=bias_sb[:, 4 * s + t : 4 * s + t + 1], scale=1.0,
-                    )
-            live[("h", n)] = acts
+            if ("h", n, s) not in live:
+                live[("h", n, s)] = rot.tile([P, 4, 512], F32, name="hs%d" % s, tag="hs%d" % s, bufs=3)
+            hs = live[("h", n, s)]
+            pre = psum.tile([P, 512], F32, name="pre", tag="pre", bufs=3)
+            nc.tensor.matmul_mx(
+                out=pre,
+                lhsT=wc[:, s, t, 0:P].bitcast(FP8X4), lhsT_scale=ws[:, s, t, 0:P],
+                rhs=a_c[:, s, 512 * b : 512 * (b + 1)].bitcast(FP8X4),
+                rhs_scale=a_s[:, s, 512 * b : 512 * (b + 1)],
+                start=True, stop=False,
+            )
+            nc.tensor.matmul_mx(
+                out=pre,
+                lhsT=wc[:, s, t, P : 2 * P].bitcast(FP8X4), lhsT_scale=ws[:, s, t, P : 2 * P],
+                rhs=b_c[:, s, :].bitcast(FP8X4), rhs_scale=b_s[:, s, :],
+                start=False, stop=True,
+            )
+            nc.scalar.activation(
+                out=hs[:, t, :], in_=pre, func=ACT.Tanh,
+                bias=bias_sb[:, 4 * s + t : 4 * s + t + 1], scale=1.0,
+            )
 
-        def mix(n):
-            hu, hp = live[("h", n)]
-            nc.vector.scalar_tensor_tensor(
-                out=hp.rearrange("p t w -> p (t w)"), in0=hu.rearrange("p t w -> p (t w)"),
-                scalar=rr[:, 0:1], in1=hp.rearrange("p t w -> p (t w)"), op0=ALU.mult, op1=ALU.add,
-            )
+        def stt(n, t0, t1):
+            hu = live[("h", n, 0)][:, t0:t1, :].rearrange("p t w -> p (t w)")
+            hp = live[("h", n, 1)][:, t0:t1, :].rearrange("p t w -> p (t w)")
+            nc.vector.scalar_tensor_tensor(out=hp, in0=hu, scalar=rr[:, 0:1], in1=hp, op0=ALU.mult, op1=ALU.add)
+
+        def scale_regroup(n):
+            hp = live[("h", n, 1)]
             st = rot.tile([P, 512, 4], BF16, name="st", tag="st", bufs=2, align_bytes=64)
-            nc.vector.tensor_scalar(
-                out=st, in0=hp.rearrange("p t w -> p w t"), scalar1=c1[:, 0:1], scalar2=None, op0=ALU.mult
-            )
+            live[("st", n)] = st
+            src = hp.rearrange("p t w -> p w t")
+            if TS_ENGINE == "G":
+                nc.gpsimd.tensor_scalar(out=st, in0=src, scalar1=c1[:, 0:1], scalar2=0.0, op0=ALU.mult, op1=ALU.add)
+            else:
+                nc.vector.tensor_scalar(out=st, in0=src, scalar1=c1[:, 0:1], scalar2=None, op0=ALU.mult)
+
+        def quant_state(n):
+            st = live[("st", n)]
             s_c = rot.tile([P, 512], U32, name="s_c", tag="s_c", bufs=2, align_bytes=64)
             s_s = rot.tile([P, 512], U8, name="s_s", tag="s_s", bufs=2, align_bytes=64)
             nc.vector.quantize_mx(out=s_c.bitcast(FP8X4), scales=s_s, in_=st.rearrange("p w t -> p (w t)"))
-            zs = rot.tile([P, 4, OUT], F32, name="zs", tag="zs", bufs=3)
+            live[("sc", n)] = (s_c, s_s)
+
+        def z_matmuls(n):
+            s_c, s_s = live[("sc", n)]
             z1 = psum.tile([P, 4, P], F32, name="z1", tag="z1", bufs=1)
+            z5s = []
             for r in range(4):
                 z5 = psum.tile([P, 512], F32, name="z5", tag="z5", bufs=4)
+                z5s.append(z5)
                 cols = slice(P * r, P * (r + 1))
                 nc.tensor.matmul_mx(
                     out=z5, lhsT=s_c[:, cols].bitcast(FP8X4), lhsT_scale=s_s[:, cols],
@@ -208,36 +237,93 @@ def tile_stateencoder_pa_kernel(
                     out=z1[:, r, :], lhsT=s_c[:, cols].bitcast(FP8X4), lhsT_scale=s_s[:, cols],
                     rhs=w2c[:, 512:640].bitcast(FP8X4), rhs_scale=w2s[:, 512:640], start=True, stop=True,
                 )
-                nc.vector.tensor_tensor(out=zs[:, r, 0:512], in0=z5, in1=b2b[:, 0:512], op=ALU.add)
+            live[("z", n)] = (z1, z5s)
+
+        def add_b2(n):
+            z1, z5s = live[("z", n)]
+            zs = rot.tile([P, 4, OUT], F32, name="zs", tag="zs", bufs=3)
+            live[("zs", n)] = zs
             nc.vector.tensor_tensor(
                 out=zs[:, :, 512:640], in0=z1,
                 in1=b2b[:, 512:640].unsqueeze(1).to_broadcast([P, 4, P]), op=ALU.add,
             )
-            live[("z", n)] = zs
-
-        def finish(n):
-            zs = live[("z", n)]
             for r in range(4):
-                nc.scalar.activation(out=zs[:, r, :], in_=zs[:, r, :], func=ACT.Tanh)
-                row0 = 512 * n + P * r
-                nc.sync.dma_start(out=out_rows[row0 : row0 + P, :], in_=zs[:, r, :])
+                nc.vector.tensor_tensor(out=zs[:, r, 0:512], in0=z5s[r], in1=b2b[:, 0:512], op=ALU.add)
 
-        prep_x(0)
-        prep_w(0, 0)
+        def finish(n, r):
+            zs = live[("zs", n)]
+            nc.scalar.activation(out=zs[:, r, :], in_=zs[:, r, :], func=ACT.Tanh)
+            row0 = 512 * n + P * r
+            nc.sync.dma_start(out=out_rows[row0 : row0 + P, :], in_=zs[:, r, :])
+
+        x_chain(0)
+        btp = psum.tile([P, P], BF16, name="btp", tag="pre", bufs=3)
+        nc.tensor.transpose(btp, bt, ident)
+        nc.vector.tensor_copy(out=bias_sb, in_=btp[:, 0:8])
+        regroup_w(0, 0, "S")
+        regroup_w(0, 1, "G")
         build_b(0, [0])
-        for c in range(1, 4):
-            prep_w(0, c)
-        prep_x(1)
+        nc.vector.tensor_tensor(out=dd, in0=mw[:, 0:1], in1=mw[:, 1:2], op=ALU.subtract)
+        nc.vector.tensor_scalar(out=dd, in0=dd, scalar1=30.0, scalar2=-30.0, op0=ALU.min, op1=ALU.max)
+        nc.scalar.activation(out=rr, in_=dd, func=ACT.Exp)
+        quant_w(0, 0)
+        quant_w(0, 1)
+        x_chain(1)
         build_b(0, [1])
-        for c in range(4):
-            prep_w(1, c)
-        prep_w2()
-        for n in range(NT + 2):
+        regroup_w(0, 3, "G")
+        regroup_w(0, 2, "V")
+        quant_w(0, 2)
+        quant_w(0, 3)
+        regroup_w(1, 0, "V")
+        regroup_w(1, 1, "G")
+        quant_w(1, 0)
+        quant_w(1, 1)
+        regroup_w(1, 2, "V")
+        regroup_w(1, 3, "G")
+        quant_w(1, 2)
+        quant_w(1, 3)
+        nc.vector.tensor_scalar(out=den, in0=rr, scalar1=1.0, scalar2=None, op0=ALU.add)
+        nc.vector.reciprocal(out=w1, in_=den)
+        nc.vector.tensor_tensor(out=c1, in0=w1, in1=gm, op=ALU.mult)
+        nc.gpsimd.tensor_scalar(
+            out=w2g, in0=w2_raw.rearrange("p k n -> p n k"), scalar1=1.0, scalar2=0.0, op0=ALU.mult, op1=ALU.add
+        )
+
+        for n in range(NT + LAG):
             if n + 1 < NT:
                 build_b(n + 1, [0, 1])
-            if n < NT:
-                hidden(n)
-            if 0 <= n - 1 < NT:
-                mix(n - 1)
-            if 0 <= n - 2 < NT:
-                finish(n - 2)
+            if n == 1:
+                x_rest(0)
+                x_rest(1)
+            if n >= NT:
+                if n - 2 < NT:
+                    z_matmuls(n - 2)
+                    add_b2(n - 2)
+                if n - 1 < NT:
+                    quant_state(n - 1)
+                for r in range(4):
+                    finish(n - LAG, r)
+                continue
+            for k in range(8):
+                if k == Z_POS:
+                    if n - 2 >= 0:
+                        z_matmuls(n - 2)
+                        add_b2(n - 2)
+                    if n - 1 >= 0:
+                        quant_state(n - 1)
+                s, t = divmod(k, 4)
+                pre_act(n, s, t)
+                if s == 1:
+                    for t0, t1 in STT_PIECES:
+                        if t1 == t + 1:
+                            stt(n, t0, t1)
+                    if t == 3:
+                        scale_regroup(n)
+                if n - LAG >= 0 and k in FINAL_SLOTS:
+                    finish(n - LAG, FINAL_SLOTS.index(k))
+            if n == 0:
+                flat = w2g.rearrange("p n k -> p (n k)")
+                nc.vector.quantize_mx(out=w2c[:, 0:512].bitcast(FP8X4), scales=w2s[:, 0:512], in_=flat[:, 0:2048])
+                nc.vector.quantize_mx(
+                    out=w2c[:, 512:640].bitcast(FP8X4), scales=w2s[:, 512:640], in_=flat[:, 2048:2560]
+                )

@@ -18,7 +18,7 @@ IB = 8
 NT = B * (L // IB)
 FLOPS = 4 * 2 * (B * L) * D * H + 2 * (B * L * L) * H * OUT
 PINNED = True
-TS_ENGINE = "G"
+TS_ON_VECTOR = (0,)
 LAG = 3
 Z_POS = 3
 FINAL_SLOTS = (2, 4, 6, 7)
@@ -128,9 +128,12 @@ def tile_stateencoder_pa_kernel(
             quant_x4(s, 0, 32)
             build_a(s, 0)
 
-        def x_rest(s):
-            copy_x4(s, 32, 128)
+        def x_rest_b0(s):
+            copy_x4(s, 32, 64)
             quant_x4(s, 32, 64)
+
+        def x_rest_b1(s):
+            copy_x4(s, 64, 128)
             quant_x4(s, 64, 128)
             build_a(s, 1)
 
@@ -209,7 +212,7 @@ def tile_stateencoder_pa_kernel(
             st = rot.tile([P, 512, 4], BF16, name="st", tag="st", bufs=2, align_bytes=64)
             live[("st", n)] = st
             src = hp.rearrange("p t w -> p w t")
-            if TS_ENGINE == "G":
+            if n not in TS_ON_VECTOR:
                 nc.gpsimd.tensor_scalar(out=st, in0=src, scalar1=c1[:, 0:1], scalar2=0.0, op0=ALU.mult, op1=ALU.add)
             else:
                 nc.vector.tensor_scalar(out=st, in0=src, scalar1=c1[:, 0:1], scalar2=None, op0=ALU.mult)
@@ -261,40 +264,29 @@ def tile_stateencoder_pa_kernel(
         nc.tensor.transpose(btp, bt, ident)
         nc.vector.tensor_copy(out=bias_sb, in_=btp[:, 0:8])
         regroup_w(0, 0, "S")
-        regroup_w(0, 1, "G")
+        regroup_w(0, 1, "V")
         build_b(0, [0])
-        nc.vector.tensor_tensor(out=dd, in0=mw[:, 0:1], in1=mw[:, 1:2], op=ALU.subtract)
-        nc.vector.tensor_scalar(out=dd, in0=dd, scalar1=30.0, scalar2=-30.0, op0=ALU.min, op1=ALU.max)
-        nc.scalar.activation(out=rr, in_=dd, func=ACT.Exp)
         quant_w(0, 0)
         quant_w(0, 1)
-        x_chain(1)
-        build_b(0, [1])
-        regroup_w(0, 3, "G")
-        regroup_w(0, 2, "V")
+        regroup_w(0, 2, "S")
+        regroup_w(0, 3, "V")
         quant_w(0, 2)
         quant_w(0, 3)
+        nc.vector.tensor_tensor(out=dd, in0=mw[:, 0:1], in1=mw[:, 1:2], op=ALU.subtract)
+        nc.vector.tensor_scalar(out=dd, in0=dd, scalar1=30.0, scalar2=-30.0, op0=ALU.min, op1=ALU.max)
+        x_chain(1)
+        build_b(0, [1])
         regroup_w(1, 0, "V")
-        regroup_w(1, 1, "G")
         quant_w(1, 0)
-        quant_w(1, 1)
-        regroup_w(1, 2, "V")
-        regroup_w(1, 3, "G")
-        quant_w(1, 2)
-        quant_w(1, 3)
-        nc.vector.tensor_scalar(out=den, in0=rr, scalar1=1.0, scalar2=None, op0=ALU.add)
-        nc.vector.reciprocal(out=w1, in_=den)
-        nc.vector.tensor_tensor(out=c1, in0=w1, in1=gm, op=ALU.mult)
-        nc.gpsimd.tensor_scalar(
-            out=w2g, in0=w2_raw.rearrange("p k n -> p n k"), scalar1=1.0, scalar2=0.0, op0=ALU.mult, op1=ALU.add
-        )
 
         for n in range(NT + LAG):
-            if n + 1 < NT:
+            if 0 < n and n + 1 < NT:
                 build_b(n + 1, [0, 1])
             if n == 1:
-                x_rest(0)
-                x_rest(1)
+                x_rest_b0(0)
+                x_rest_b0(1)
+            if n in (5, 6):
+                x_rest_b1(n - 5)
             if n >= NT:
                 if n - 2 < NT:
                     z_matmuls(n - 2)
@@ -312,6 +304,18 @@ def tile_stateencoder_pa_kernel(
                     if n - 1 >= 0:
                         quant_state(n - 1)
                 s, t = divmod(k, 4)
+                if n == 0 and k == 4:
+                    nc.scalar.activation(out=rr, in_=dd, func=ACT.Exp)
+                    regroup_w(1, 1, "S")
+                    regroup_w(1, 2, "V")
+                    quant_w(1, 1)
+                    quant_w(1, 2)
+                    regroup_w(1, 3, "V")
+                    quant_w(1, 3)
+                    build_b(1, [0, 1])
+                    nc.vector.tensor_scalar(out=den, in0=rr, scalar1=1.0, scalar2=None, op0=ALU.add)
+                    nc.vector.reciprocal(out=w1, in_=den)
+                    nc.vector.tensor_tensor(out=c1, in0=w1, in1=gm, op=ALU.mult)
                 pre_act(n, s, t)
                 if s == 1:
                     for t0, t1 in STT_PIECES:
@@ -322,6 +326,7 @@ def tile_stateencoder_pa_kernel(
                 if n - LAG >= 0 and k in FINAL_SLOTS:
                     finish(n - LAG, FINAL_SLOTS.index(k))
             if n == 0:
+                nc.vector.tensor_copy(out=w2g, in_=w2_raw.rearrange("p k n -> p n k"))
                 flat = w2g.rearrange("p n k -> p (n k)")
                 nc.vector.quantize_mx(out=w2c[:, 0:512].bitcast(FP8X4), scales=w2s[:, 0:512], in_=flat[:, 0:2048])
                 nc.vector.quantize_mx(

@@ -19,6 +19,7 @@ NT = B * (L // IB)
 FLOPS = 4 * 2 * (B * L) * D * H + 2 * (B * L * L) * H * OUT
 PINNED = True
 TS_ON_VECTOR = (0,)
+G_COLS = 384
 LAG = 3
 Z_POS = 3
 FINAL_SLOTS = (2, 4, 6, 7)
@@ -211,14 +212,26 @@ def tile_stateencoder_pa_kernel(
             hp = live[("h", n, 1)]
             st = rot.tile([P, 512, 4], BF16, name="st", tag="st", bufs=2, align_bytes=64)
             live[("st", n)] = st
-            src = hp.rearrange("p t w -> p w t")
             if n not in TS_ON_VECTOR:
-                nc.gpsimd.tensor_scalar(out=st, in0=src, scalar1=c1[:, 0:1], scalar2=0.0, op0=ALU.mult, op1=ALU.add)
+                nc.gpsimd.tensor_scalar(
+                    out=st[:, 0:G_COLS, :], in0=hp[:, :, 0:G_COLS].rearrange("p t w -> p w t"),
+                    scalar1=c1[:, 0:1], scalar2=0.0, op0=ALU.mult, op1=ALU.add,
+                )
             else:
-                nc.vector.tensor_scalar(out=st, in0=src, scalar1=c1[:, 0:1], scalar2=None, op0=ALU.mult)
+                scale_regroup_v(n, 0)
+
+        def scale_regroup_v(n, w0):
+            hp = live[("h", n, 1)]
+            st = live[("st", n)]
+            nc.vector.tensor_scalar(
+                out=st[:, w0:512, :], in0=hp[:, :, w0:512].rearrange("p t w -> p w t"),
+                scalar1=c1[:, 0:1], scalar2=None, op0=ALU.mult,
+            )
 
         def quant_state(n):
             st = live[("st", n)]
+            if n not in TS_ON_VECTOR:
+                scale_regroup_v(n, G_COLS)
             s_c = rot.tile([P, 512], U32, name="s_c", tag="s_c", bufs=2, align_bytes=64)
             s_s = rot.tile([P, 512], U8, name="s_s", tag="s_s", bufs=2, align_bytes=64)
             nc.vector.quantize_mx(out=s_c.bitcast(FP8X4), scales=s_s, in_=st.rearrange("p w t -> p (w t)"))

@@ -17,9 +17,8 @@ B, L, D, H, OUT = 2, 64, 512, 512, 640
 IB = 8
 NT = B * (L // IB)
 FLOPS = 4 * 2 * (B * L) * D * H + 2 * (B * L * L) * H * OUT
-PINNED = True
+PINNED = False
 TS_ON_VECTOR = (0,)
-G_COLS = 384
 LAG = 3
 Z_POS = 3
 FINAL_SLOTS = (2, 4, 6, 7)
@@ -67,7 +66,7 @@ def tile_stateencoder_pa_kernel(
                 cols = slice(256 * half, 256 * (half + 1))
                 nc.sync.dma_start(out=w_raw[s][:, :, cols], in_=w_view[:, :, cols])
         nc.sync.dma_start(out=w2_raw, in_=W2.rearrange("(k p) n -> p k n", p=P))
-        nc.scalar.dma_start(out=b2b, in_=b2.partition_broadcast(P))
+        nc.sync.dma_start(out=b2b, in_=b2.partition_broadcast(P))
         nc.scalar.activation(out=one1, in_=zero1, func=ACT.Exp)
 
         x1 = [keep.tile([P, P, 4], BF16, name="x1_%d" % s, align_bytes=64) for s in range(2)]
@@ -117,7 +116,7 @@ def tile_stateencoder_pa_kernel(
             )
 
         def x_chain(s):
-            xt = psum.tile([P, 4, P], BF16, name="xt", tag="pre", bufs=3)
+            xt = psum.tile([P, 4, P], BF16, name="xt", tag="pre", bufs=5)
             for t in range(4):
                 nc.tensor.transpose(xt[:, t, :], x_sb[s][:, P * t : P * (t + 1)], ident)
             nc.vector.tensor_copy(out=x1[s], in_=xt.rearrange("p t r -> p r t"))
@@ -162,8 +161,8 @@ def tile_stateencoder_pa_kernel(
         def build_b(n, streams):
             tok0 = IB * n
             if ("b", n) not in live:
-                b_c = rot.tile([P, 2, 512], U32, name="b_c", tag="b_c", bufs=2, align_bytes=64)
-                b_s = rot.tile([P, 2, 512], U8, name="b_s", tag="b_s", bufs=2, align_bytes=64)
+                b_c = rot.tile([P, 2, 512], U32, name="b_c", tag="b_c", bufs=3, align_bytes=64)
+                b_s = rot.tile([P, 2, 512], U8, name="b_s", tag="b_s", bufs=3, align_bytes=64)
                 live[("b", n)] = (b_c, b_s)
             b_c, b_s = live[("b", n)]
             s0, s1 = streams[0], streams[-1] + 1
@@ -182,9 +181,9 @@ def tile_stateencoder_pa_kernel(
             b = n // (L // IB)
             b_c, b_s = live[("b", n)]
             if ("h", n, s) not in live:
-                live[("h", n, s)] = rot.tile([P, 4, 512], F32, name="hs%d" % s, tag="hs%d" % s, bufs=3)
+                live[("h", n, s)] = rot.tile([P, 4, 512], F32, name="hs%d" % s, tag="hs%d" % s, bufs=4)
             hs = live[("h", n, s)]
-            pre = psum.tile([P, 512], F32, name="pre", tag="pre", bufs=3)
+            pre = psum.tile([P, 512], F32, name="pre", tag="pre", bufs=5)
             nc.tensor.matmul_mx(
                 out=pre,
                 lhsT=wc[:, s, t, 0:P].bitcast(FP8X4), lhsT_scale=ws[:, s, t, 0:P],
@@ -212,28 +211,16 @@ def tile_stateencoder_pa_kernel(
             hp = live[("h", n, 1)]
             st = rot.tile([P, 512, 4], BF16, name="st", tag="st", bufs=2, align_bytes=64)
             live[("st", n)] = st
+            src = hp.rearrange("p t w -> p w t")
             if n not in TS_ON_VECTOR:
-                nc.gpsimd.tensor_scalar(
-                    out=st[:, 0:G_COLS, :], in0=hp[:, :, 0:G_COLS].rearrange("p t w -> p w t"),
-                    scalar1=c1[:, 0:1], scalar2=0.0, op0=ALU.mult, op1=ALU.add,
-                )
+                nc.gpsimd.tensor_scalar(out=st, in0=src, scalar1=c1[:, 0:1], scalar2=0.0, op0=ALU.mult, op1=ALU.add)
             else:
-                scale_regroup_v(n, 0)
-
-        def scale_regroup_v(n, w0):
-            hp = live[("h", n, 1)]
-            st = live[("st", n)]
-            nc.vector.tensor_scalar(
-                out=st[:, w0:512, :], in0=hp[:, :, w0:512].rearrange("p t w -> p w t"),
-                scalar1=c1[:, 0:1], scalar2=None, op0=ALU.mult,
-            )
+                nc.vector.tensor_scalar(out=st, in0=src, scalar1=c1[:, 0:1], scalar2=None, op0=ALU.mult)
 
         def quant_state(n):
             st = live[("st", n)]
-            if n not in TS_ON_VECTOR:
-                scale_regroup_v(n, G_COLS)
-            s_c = rot.tile([P, 512], U32, name="s_c", tag="s_c", bufs=2, align_bytes=64)
-            s_s = rot.tile([P, 512], U8, name="s_s", tag="s_s", bufs=2, align_bytes=64)
+            s_c = rot.tile([P, 512], U32, name="s_c", tag="s_c", bufs=3, align_bytes=64)
+            s_s = rot.tile([P, 512], U8, name="s_s", tag="s_s", bufs=3, align_bytes=64)
             nc.vector.quantize_mx(out=s_c.bitcast(FP8X4), scales=s_s, in_=st.rearrange("p w t -> p (w t)"))
             live[("sc", n)] = (s_c, s_s)
 
@@ -242,7 +229,7 @@ def tile_stateencoder_pa_kernel(
             z1 = psum.tile([P, 4, P], F32, name="z1", tag="z1", bufs=1)
             z5s = []
             for r in range(4):
-                z5 = psum.tile([P, 512], F32, name="z5", tag="z5", bufs=4)
+                z5 = psum.tile([P, 512], F32, name="z5", tag="z5", bufs=2)
                 z5s.append(z5)
                 cols = slice(P * r, P * (r + 1))
                 nc.tensor.matmul_mx(
@@ -257,7 +244,7 @@ def tile_stateencoder_pa_kernel(
 
         def add_b2(n):
             z1, z5s = live[("z", n)]
-            zs = rot.tile([P, 4, OUT], F32, name="zs", tag="zs", bufs=3)
+            zs = rot.tile([P, 4, OUT], F32, name="zs", tag="zs", bufs=4)
             live[("zs", n)] = zs
             nc.vector.tensor_tensor(
                 out=zs[:, :, 512:640], in0=z1,
@@ -273,7 +260,7 @@ def tile_stateencoder_pa_kernel(
             nc.sync.dma_start(out=out_rows[row0 : row0 + P, :], in_=zs[:, r, :])
 
         x_chain(0)
-        btp = psum.tile([P, P], BF16, name="btp", tag="pre", bufs=3)
+        btp = psum.tile([P, P], BF16, name="btp", tag="pre", bufs=5)
         nc.tensor.transpose(btp, bt, ident)
         nc.vector.tensor_copy(out=bias_sb, in_=btp[:, 0:8])
         regroup_w(0, 0, "S")

@@ -17,11 +17,10 @@ B, L, D, H, OUT = 2, 64, 512, 512, 640
 IB = 8
 NT = B * (L // IB)
 FLOPS = 4 * 2 * (B * L) * D * H + 2 * (B * L * L) * H * OUT
-PINNED = False
+PINNED = True
 TS_ON_VECTOR = (0,)
 LAG = 3
 Z_POS = 3
-FINAL_SLOTS = (2, 4, 6, 7)
 STT_PIECES = ((0, 2), (2, 3), (3, 4))
 
 
@@ -116,7 +115,7 @@ def tile_stateencoder_pa_kernel(
             )
 
         def x_chain(s):
-            xt = psum.tile([P, 4, P], BF16, name="xt", tag="pre", bufs=5)
+            xt = psum.tile([P, 4, P], BF16, name="xt", tag="pre", bufs=3)
             for t in range(4):
                 nc.tensor.transpose(xt[:, t, :], x_sb[s][:, P * t : P * (t + 1)], ident)
             nc.vector.tensor_copy(out=x1[s], in_=xt.rearrange("p t r -> p r t"))
@@ -161,8 +160,8 @@ def tile_stateencoder_pa_kernel(
         def build_b(n, streams):
             tok0 = IB * n
             if ("b", n) not in live:
-                b_c = rot.tile([P, 2, 512], U32, name="b_c", tag="b_c", bufs=3, align_bytes=64)
-                b_s = rot.tile([P, 2, 512], U8, name="b_s", tag="b_s", bufs=3, align_bytes=64)
+                b_c = rot.tile([P, 2, 512], U32, name="b_c", tag="b_c", bufs=2, align_bytes=64)
+                b_s = rot.tile([P, 2, 512], U8, name="b_s", tag="b_s", bufs=2, align_bytes=64)
                 live[("b", n)] = (b_c, b_s)
             b_c, b_s = live[("b", n)]
             s0, s1 = streams[0], streams[-1] + 1
@@ -181,9 +180,9 @@ def tile_stateencoder_pa_kernel(
             b = n // (L // IB)
             b_c, b_s = live[("b", n)]
             if ("h", n, s) not in live:
-                live[("h", n, s)] = rot.tile([P, 4, 512], F32, name="hs%d" % s, tag="hs%d" % s, bufs=4)
+                live[("h", n, s)] = rot.tile([P, 4, 512], F32, name="hs%d" % s, tag="hs%d" % s, bufs=3)
             hs = live[("h", n, s)]
-            pre = psum.tile([P, 512], F32, name="pre", tag="pre", bufs=5)
+            pre = psum.tile([P, 512], F32, name="pre", tag="pre", bufs=3)
             nc.tensor.matmul_mx(
                 out=pre,
                 lhsT=wc[:, s, t, 0:P].bitcast(FP8X4), lhsT_scale=ws[:, s, t, 0:P],
@@ -219,8 +218,8 @@ def tile_stateencoder_pa_kernel(
 
         def quant_state(n):
             st = live[("st", n)]
-            s_c = rot.tile([P, 512], U32, name="s_c", tag="s_c", bufs=3, align_bytes=64)
-            s_s = rot.tile([P, 512], U8, name="s_s", tag="s_s", bufs=3, align_bytes=64)
+            s_c = rot.tile([P, 512], U32, name="s_c", tag="s_c", bufs=2, align_bytes=64)
+            s_s = rot.tile([P, 512], U8, name="s_s", tag="s_s", bufs=2, align_bytes=64)
             nc.vector.quantize_mx(out=s_c.bitcast(FP8X4), scales=s_s, in_=st.rearrange("p w t -> p (w t)"))
             live[("sc", n)] = (s_c, s_s)
 
@@ -229,7 +228,7 @@ def tile_stateencoder_pa_kernel(
             z1 = psum.tile([P, 4, P], F32, name="z1", tag="z1", bufs=1)
             z5s = []
             for r in range(4):
-                z5 = psum.tile([P, 512], F32, name="z5", tag="z5", bufs=2)
+                z5 = psum.tile([P, 512], F32, name="z5", tag="z5", bufs=4)
                 z5s.append(z5)
                 cols = slice(P * r, P * (r + 1))
                 nc.tensor.matmul_mx(
@@ -244,7 +243,7 @@ def tile_stateencoder_pa_kernel(
 
         def add_b2(n):
             z1, z5s = live[("z", n)]
-            zs = rot.tile([P, 4, OUT], F32, name="zs", tag="zs", bufs=4)
+            zs = rot.tile([P, 4, OUT], F32, name="zs", tag="zs", bufs=3)
             live[("zs", n)] = zs
             nc.vector.tensor_tensor(
                 out=zs[:, :, 512:640], in0=z1,
@@ -260,7 +259,7 @@ def tile_stateencoder_pa_kernel(
             nc.sync.dma_start(out=out_rows[row0 : row0 + P, :], in_=zs[:, r, :])
 
         x_chain(0)
-        btp = psum.tile([P, P], BF16, name="btp", tag="pre", bufs=5)
+        btp = psum.tile([P, P], BF16, name="btp", tag="pre", bufs=3)
         nc.tensor.transpose(btp, bt, ident)
         nc.vector.tensor_copy(out=bias_sb, in_=btp[:, 0:8])
         regroup_w(0, 0, "S")
@@ -323,8 +322,9 @@ def tile_stateencoder_pa_kernel(
                             stt(n, t0, t1)
                     if t == 3:
                         scale_regroup(n)
-                if n - LAG >= 0 and k in FINAL_SLOTS:
-                    finish(n - LAG, FINAL_SLOTS.index(k))
+                if n - LAG >= 0 and k == 7:
+                    for r in range(4):
+                        finish(n - LAG, r)
             if n == 0:
                 nc.vector.tensor_copy(out=w2g, in_=w2_raw.rearrange("p k n -> p n k"))
                 flat = w2g.rearrange("p n k -> p (n k)")

@@ -19,8 +19,7 @@ NT = B * (L // IB)
 FLOPS = 4 * 2 * (B * L) * D * H + 2 * (B * L * L) * H * OUT
 PINNED = True
 TS_ON_VECTOR = (0,)
-LAG = 3
-Z_POS = 3
+LAG = 2
 STT_PIECES = ((0, 2), (2, 3), (3, 4))
 
 
@@ -278,53 +277,34 @@ def tile_stateencoder_pa_kernel(
         regroup_w(1, 0, "V")
         quant_w(1, 0)
 
+        build_b(1, [0])
         for n in range(NT + LAG):
-            if 0 < n and n + 1 < NT:
-                build_b(n + 1, [0, 1])
-            if n == 1:
-                x_rest_b0(0)
-                x_rest_b0(1)
-            if n in (5, 6):
-                x_rest_b1(n - 5)
-            if n >= NT:
-                if n - 2 < NT:
-                    z_matmuls(n - 2)
-                    add_b2(n - 2)
-                if n - 1 < NT:
-                    quant_state(n - 1)
-                for r in range(4):
-                    finish(n - LAG, r)
-                continue
-            for k in range(8):
-                if k == Z_POS:
-                    if n - 2 >= 0:
-                        z_matmuls(n - 2)
-                        add_b2(n - 2)
-                    if n - 1 >= 0:
-                        quant_state(n - 1)
-                s, t = divmod(k, 4)
-                if n == 0 and k == 4:
-                    nc.scalar.activation(out=rr, in_=dd, func=ACT.Exp)
-                    regroup_w(1, 1, "S")
-                    regroup_w(1, 2, "V")
-                    quant_w(1, 1)
-                    quant_w(1, 2)
-                    regroup_w(1, 3, "V")
-                    quant_w(1, 3)
-                    build_b(1, [0, 1])
-                    nc.vector.tensor_scalar(out=den, in0=rr, scalar1=1.0, scalar2=None, op0=ALU.add)
-                    nc.vector.reciprocal(out=w1, in_=den)
-                    nc.vector.tensor_tensor(out=c1, in0=w1, in1=gm, op=ALU.mult)
-                pre_act(n, s, t)
-                if s == 1:
-                    for t0, t1 in STT_PIECES:
-                        if t1 == t + 1:
-                            stt(n, t0, t1)
-                    if t == 3:
-                        scale_regroup(n)
-                if n - LAG >= 0 and k == 7:
-                    for r in range(4):
-                        finish(n - LAG, r)
+            if n < NT:
+                for k in range(8):
+                    s, t = divmod(k, 4)
+                    if n == 0 and k == 4:
+                        nc.scalar.activation(out=rr, in_=dd, func=ACT.Exp)
+                        regroup_w(1, 1, "S")
+                        regroup_w(1, 2, "V")
+                        quant_w(1, 1)
+                        quant_w(1, 2)
+                        regroup_w(1, 3, "V")
+                        quant_w(1, 3)
+                        build_b(1, [1])
+                        nc.vector.tensor_scalar(out=den, in0=rr, scalar1=1.0, scalar2=None, op0=ALU.add)
+                        nc.vector.reciprocal(out=w1, in_=den)
+                        nc.vector.tensor_tensor(out=c1, in0=w1, in1=gm, op=ALU.mult)
+                    pre_act(n, s, t)
+                    if s == 1:
+                        for t0, t1 in STT_PIECES:
+                            if t1 == t + 1:
+                                stt(n, t0, t1)
+            if 0 <= n - 1 < NT:
+                z_matmuls(n - 1)
+            if n < NT:
+                scale_regroup(n)
+            if 0 <= n - 1 < NT:
+                add_b2(n - 1)
             if n == 0:
                 nc.vector.tensor_copy(out=w2g, in_=w2_raw.rearrange("p k n -> p n k"))
                 flat = w2g.rearrange("p n k -> p (n k)")
@@ -332,3 +312,15 @@ def tile_stateencoder_pa_kernel(
                 nc.vector.quantize_mx(
                     out=w2c[:, 512:640].bitcast(FP8X4), scales=w2s[:, 512:640], in_=flat[:, 2048:2560]
                 )
+            if n < NT:
+                quant_state(n)
+            if n == 1:
+                x_rest_b0(0)
+                x_rest_b0(1)
+            if n in (4, 5):
+                x_rest_b1(n - 4)
+            if n + 2 < NT:
+                build_b(n + 2, [0, 1])
+            if n - LAG >= 0:
+                for r in range(4):
+                    finish(n - LAG, r)

@@ -14,13 +14,13 @@ ALU = mybir.AluOpType
 
 P = 128
 B, L, D, H, OUT = 2, 64, 512, 512, 640
-IB = 8
-NT = B * (L // IB)
+TI, TJ = 16, 32
+NT = B * L * L // 512
+NM = NT // 2
 FLOPS = 4 * 2 * (B * L) * D * H + 2 * (B * L * L) * H * OUT
-PINNED = True
-TS_ON_VECTOR = (0,)
-LAG = 2
-STT_PIECES = ((0, 2), (2, 3), (3, 4))
+SCALE_ON_VECTOR = (0, 1, NT - 1)
+LAG = 3
+AHEAD = 2
 
 
 def tile_stateencoder_pa_kernel(
@@ -32,8 +32,7 @@ def tile_stateencoder_pa_kernel(
         keep = ctx.enter_context(tc.tile_pool(name="keep", bufs=1))
         rot = ctx.enter_context(tc.tile_pool(name="rot", bufs=2))
         psum = ctx.enter_context(tc.psum_pool(name="psum", bufs=1))
-        if PINNED:
-            ctx.enter_context(tc.manual_schedule())
+        ctx.enter_context(tc.manual_schedule())
 
         x_in = [global_outputs, sp_outputs]
         w_in = [W_utt, W_sp]
@@ -52,29 +51,28 @@ def tile_stateencoder_pa_kernel(
         nc.gpsimd.memset(zero1, 0.0)
         make_identity(nc, ident)
         with nc.allow_non_contiguous_dma(reason="small vectors"):
-            nc.scalar.dma_start(out=bt[0:4, :], in_=b_utt.rearrange("(t p) -> t p", p=P))
-            nc.scalar.dma_start(out=bt[4:8, :], in_=b_sp.rearrange("(t p) -> t p", p=P))
             nc.scalar.dma_start(out=mw, in_=mix_w.partition_broadcast(P))
             nc.scalar.dma_start(out=gm, in_=gamma.partition_broadcast(P))
         for s in range(2):
             nc.sync.dma_start(out=x_sb[s], in_=x_in[s].rearrange("b l d -> (b l) d"))
         for s in range(2):
+            nc.sync.dma_start(out=bt[4 * s : 4 * s + 4, :], in_=[b_utt, b_sp][s].rearrange("(t p) -> t p", p=P))
+        for s in range(2):
             w_view = w_in[s].rearrange("(s p) n -> p s n", p=P)
-            for half in range(2):
-                cols = slice(256 * half, 256 * (half + 1))
+            pieces = 2 - s
+            for piece in range(pieces):
+                cols = slice(H * piece // pieces, H * (piece + 1) // pieces)
                 nc.sync.dma_start(out=w_raw[s][:, :, cols], in_=w_view[:, :, cols])
         nc.sync.dma_start(out=w2_raw, in_=W2.rearrange("(k p) n -> p k n", p=P))
         nc.sync.dma_start(out=b2b, in_=b2.partition_broadcast(P))
         nc.scalar.activation(out=one1, in_=zero1, func=ACT.Exp)
 
-        x1 = [keep.tile([P, P, 4], BF16, name="x1_%d" % s, align_bytes=64) for s in range(2)]
-        x4 = [keep.tile([P, P, 4, 4], BF16, name="x4_%d" % s, align_bytes=64) for s in range(2)]
+        x1 = keep.tile([P, 2, P, 4], BF16, name="x1", align_bytes=64)
         xc1 = keep.tile([P, 2, P], U32, name="xc1", align_bytes=64)
         xs1 = keep.tile([P, 2, P], U8, name="xs1", align_bytes=64)
-        xc4 = keep.tile([P, 2, 4 * P], U32, name="xc4", align_bytes=64)
-        xs4 = keep.tile([P, 2, 4 * P], U8, name="xs4", align_bytes=64)
-        a_c = keep.tile([P, 2, 1024], U32, name="a_c", align_bytes=64)
-        a_s = keep.tile([P, 2, 1024], U8, name="a_s", align_bytes=64)
+        xs4 = keep.tile([P, NM, 2, 4 * TI], U8, name="xs4", align_bytes=64)
+        a_c = keep.tile([P, 2, B, 2, 512], U32, name="a_c", align_bytes=64)
+        a_s = keep.tile([P, 2, B, 2, 512], U8, name="a_s", align_bytes=64)
         wc = keep.tile([P, 2, 4, 256], U32, name="wc", align_bytes=64)
         ws = keep.tile([P, 2, 4, 256], U8, name="ws", align_bytes=64)
         w2g = keep.tile([P, OUT, 4], BF16, name="w2g", align_bytes=64)
@@ -86,66 +84,80 @@ def tile_stateencoder_pa_kernel(
         den = keep.tile([P, 1], F32, name="den")
         w1 = keep.tile([P, 1], F32, name="w1")
         c1 = keep.tile([P, 1], F32, name="c1")
-        xs4_words = xs4.rearrange("p s c -> p (s c)").bitcast(I32).rearrange("p (s k) -> p s k", s=2)
+        xs1_words = xs1.rearrange("p s c -> p (s c)").bitcast(I32).rearrange("p (s w) -> p s w", s=2)
+        xs4_words = xs4.rearrange("p m s c -> p (m s c)").bitcast(I32).rearrange("p (m s k) -> p m s k", m=NM, s=2)
+        a_words = (
+            a_s.rearrange("p s b h c -> p (s b h c)").bitcast(I32)
+            .rearrange("p (s b h r w) -> p s b h r w", s=2, b=B, h=2, r=TI)
+        )
 
         nc.vector.memset(xs1.rearrange("p s c -> p (s c)").bitcast(I32), 0)
-        nc.vector.memset(xs4.rearrange("p s c -> p (s c)").bitcast(I32), 0)
+        nc.vector.memset(xs4.rearrange("p m s c -> p (m s c)").bitcast(I32), 0)
 
-        def quant_x4(s, tok0, tok1):
-            nc.vector.quantize_mx(
-                out=xc4[:, s, 4 * tok0 : 4 * tok1].bitcast(FP8X4), scales=xs4[:, s, 4 * tok0 : 4 * tok1],
-                in_=x4[s][:, tok0:tok1].rearrange("p r c t -> p (r c t)"),
-            )
+        live = {}
+        w_grouped = {}
 
-        def copy_x4(s, tok0, tok1):
-            nc.vector.tensor_copy(
-                out=x4[s][:, tok0:tok1],
-                in_=x1[s][:, tok0:tok1].unsqueeze(2).to_broadcast([P, tok1 - tok0, 4, 4]),
-            )
-
-        def build_a(s, b):
-            nc.vector.tensor_copy(
-                out=a_c[:, s, 512 * b : 512 * (b + 1)].bitcast(I32).rearrange("p (r j) -> p r j", r=IB),
-                in_=xc1[:, s, L * b : L * (b + 1)].bitcast(I32).unsqueeze(1).to_broadcast([P, IB, L]),
-            )
-            nc.vector.tensor_copy(
-                out=a_s[:, s, 512 * b : 512 * (b + 1)].bitcast(I32).rearrange("p (r w) -> p r w", r=IB),
-                in_=xs1[:, s, L * b : L * (b + 1)].bitcast(I32).unsqueeze(1).to_broadcast([P, IB, L // 4]),
-            )
-
-        def x_chain(s):
+        def x_transposes(s):
             xt = psum.tile([P, 4, P], BF16, name="xt", tag="pre", bufs=3)
             for t in range(4):
                 nc.tensor.transpose(xt[:, t, :], x_sb[s][:, P * t : P * (t + 1)], ident)
-            nc.vector.tensor_copy(out=x1[s], in_=xt.rearrange("p t r -> p r t"))
+            live[("xt", s)] = xt
+
+        def x_codes(s, copy):
+            copy(out=x1[:, s], in_=live[("xt", s)].rearrange("p t r -> p r t"))
             nc.vector.quantize_mx(
                 out=xc1[:, s, :].bitcast(FP8X4), scales=xs1[:, s, :],
-                in_=x1[s].rearrange("p r t -> p (r t)"),
+                in_=x1[:, s].rearrange("p r t -> p (r t)"),
             )
-            copy_x4(s, 0, 32)
-            quant_x4(s, 0, 32)
-            build_a(s, 0)
 
-        def x_rest_b0(s):
-            copy_x4(s, 32, 64)
-            quant_x4(s, 32, 64)
+        def copy_x4(m, s0, s1):
+            if ("x4", m) not in live:
+                live[("x4", m)] = rot.tile([P, 2, TI, 4, 4], BF16, name="x4", tag="x4", bufs=2, align_bytes=64)
+            nc.vector.tensor_copy(
+                out=live[("x4", m)][:, s0:s1],
+                in_=x1[:, s0:s1, TI * m : TI * (m + 1), :].unsqueeze(3).to_broadcast([P, s1 - s0, TI, 4, 4]),
+            )
 
-        def x_rest_b1(s):
-            copy_x4(s, 64, 128)
-            quant_x4(s, 64, 128)
-            build_a(s, 1)
+        def quant_x4(m, s0, s1):
+            xc4 = rot.tile([P, 2, 4 * TI], U32, name="xc4", tag="xc4", bufs=2, align_bytes=64)
+            nc.vector.quantize_mx(
+                out=xc4[:, s0:s1].rearrange("p s c -> p (s c)").bitcast(FP8X4),
+                scales=xs4[:, m, s0:s1].rearrange("p s c -> p (s c)"),
+                in_=live[("x4", m)][:, s0:s1].rearrange("p s i c t -> p (s i c t)"),
+            )
 
-        w_grouped = {}
+        def build_a(b, h, s0, s1):
+            ns = s1 - s0
+            tok0 = L * b + TJ * h
+            nc.vector.tensor_copy(
+                out=a_c[:, s0:s1, b, h, :].bitcast(I32).rearrange("p s (i j) -> p s i j", i=TI),
+                in_=xc1[:, s0:s1, tok0 : tok0 + TJ].bitcast(I32).unsqueeze(2).to_broadcast([P, ns, TI, TJ]),
+            )
+            nc.vector.tensor_copy(
+                out=a_words[:, s0:s1, b, h],
+                in_=xs1_words[:, s0:s1, tok0 // 4 : (tok0 + TJ) // 4].unsqueeze(2).to_broadcast([P, ns, TI, TJ // 4]),
+            )
+
+        def build_b(m, s):
+            b_c = rot.tile([P, 512], U32, name="b_c%d" % s, tag="b_c%d" % s, bufs=2, align_bytes=64)
+            b_s = rot.tile([P, 512], U8, name="b_s%d" % s, tag="b_s%d" % s, bufs=2, align_bytes=64)
+            live[("b", m, s)] = (b_c, b_s)
+            nc.vector.tensor_copy(
+                out=b_c.bitcast(I32).rearrange("p (i j) -> p i j", i=TI),
+                in_=xc1[:, s, TI * m : TI * (m + 1)].bitcast(I32).unsqueeze(2).to_broadcast([P, TI, TJ]),
+            )
+            nc.vector.tensor_copy(
+                out=b_s.bitcast(I32).rearrange("p (i w) -> p i w", i=TI),
+                in_=xs4_words[:, m, s].unsqueeze(2).to_broadcast([P, TI, TJ // 4]),
+            )
 
         def regroup_w(s, c, engine):
             wg = rot.tile([P, 2, P, 4], BF16, name="wg", tag="wg", bufs=4, align_bytes=64)
             src = w_raw[s][:, :, P * c : P * (c + 1)].rearrange("p (g k) m -> p g m k", g=2)
             if engine == "V":
                 nc.vector.tensor_copy(out=wg, in_=src)
-            elif engine == "S":
-                nc.scalar.copy(out=wg, in_=src)
             else:
-                nc.gpsimd.tensor_scalar(out=wg, in0=src, scalar1=1.0, scalar2=0.0, op0=ALU.mult, op1=ALU.add)
+                nc.scalar.copy(out=wg, in_=src)
             w_grouped[(s, c)] = wg
 
         def quant_w(s, c):
@@ -154,45 +166,24 @@ def tile_stateencoder_pa_kernel(
                 in_=w_grouped[(s, c)].rearrange("p g m k -> p (g m k)"),
             )
 
-        live = {}
-
-        def build_b(n, streams):
-            tok0 = IB * n
-            if ("b", n) not in live:
-                b_c = rot.tile([P, 2, 512], U32, name="b_c", tag="b_c", bufs=2, align_bytes=64)
-                b_s = rot.tile([P, 2, 512], U8, name="b_s", tag="b_s", bufs=2, align_bytes=64)
-                live[("b", n)] = (b_c, b_s)
-            b_c, b_s = live[("b", n)]
-            s0, s1 = streams[0], streams[-1] + 1
-            ns = s1 - s0
-            nc.vector.tensor_copy(
-                out=b_c[:, s0:s1, :].bitcast(I32).rearrange("p s (i j) -> p s i j", i=IB),
-                in_=xc1[:, s0:s1, tok0 : tok0 + IB].bitcast(I32).unsqueeze(3).to_broadcast([P, ns, IB, L]),
-            )
-            nc.vector.tensor_copy(
-                out=b_s.rearrange("p s c -> p (s c)").bitcast(I32)
-                .rearrange("p (s i w) -> p s i w", s=2, i=IB)[:, s0:s1],
-                in_=xs4_words[:, s0:s1, tok0 : tok0 + IB].unsqueeze(3).to_broadcast([P, ns, IB, L // 4]),
-            )
-
         def pre_act(n, s, t):
-            b = n // (L // IB)
-            b_c, b_s = live[("b", n)]
+            m, h = divmod(n, 2)
+            b = m // (NM // B)
+            b_c, b_s = live[("b", m, s)]
             if ("h", n, s) not in live:
-                live[("h", n, s)] = rot.tile([P, 4, 512], F32, name="hs%d" % s, tag="hs%d" % s, bufs=3)
+                live[("h", n, s)] = rot.tile([P, 4, 512], F32, name="hs%d" % s, tag="hs%d" % s, bufs=(AHEAD + 2, 3)[s])
             hs = live[("h", n, s)]
             pre = psum.tile([P, 512], F32, name="pre", tag="pre", bufs=3)
             nc.tensor.matmul_mx(
                 out=pre,
                 lhsT=wc[:, s, t, 0:P].bitcast(FP8X4), lhsT_scale=ws[:, s, t, 0:P],
-                rhs=a_c[:, s, 512 * b : 512 * (b + 1)].bitcast(FP8X4),
-                rhs_scale=a_s[:, s, 512 * b : 512 * (b + 1)],
+                rhs=a_c[:, s, b, h, :].bitcast(FP8X4), rhs_scale=a_s[:, s, b, h, :],
                 start=True, stop=False,
             )
             nc.tensor.matmul_mx(
                 out=pre,
                 lhsT=wc[:, s, t, P : 2 * P].bitcast(FP8X4), lhsT_scale=ws[:, s, t, P : 2 * P],
-                rhs=b_c[:, s, :].bitcast(FP8X4), rhs_scale=b_s[:, s, :],
+                rhs=b_c.bitcast(FP8X4), rhs_scale=b_s,
                 start=False, stop=True,
             )
             nc.scalar.activation(
@@ -200,34 +191,39 @@ def tile_stateencoder_pa_kernel(
                 bias=bias_sb[:, 4 * s + t : 4 * s + t + 1], scale=1.0,
             )
 
-        def stt(n, t0, t1):
-            hu = live[("h", n, 0)][:, t0:t1, :].rearrange("p t w -> p (t w)")
-            hp = live[("h", n, 1)][:, t0:t1, :].rearrange("p t w -> p (t w)")
+        def mix(n, t0, t1):
+            hu = live[("h", n, 0)][:, t0:t1].rearrange("p t w -> p (t w)")
+            hp = live[("h", n, 1)][:, t0:t1].rearrange("p t w -> p (t w)")
             nc.vector.scalar_tensor_tensor(out=hp, in0=hu, scalar=rr[:, 0:1], in1=hp, op0=ALU.mult, op1=ALU.add)
 
         def scale_regroup(n):
-            hp = live[("h", n, 1)]
-            st = rot.tile([P, 512, 4], BF16, name="st", tag="st", bufs=2, align_bytes=64)
-            live[("st", n)] = st
-            src = hp.rearrange("p t w -> p w t")
-            if n not in TS_ON_VECTOR:
-                nc.gpsimd.tensor_scalar(out=st, in0=src, scalar1=c1[:, 0:1], scalar2=0.0, op0=ALU.mult, op1=ALU.add)
+            m, h = divmod(n, 2)
+            if h == 0:
+                live[("st", m)] = rot.tile([P, TI, 2, TJ, 4], BF16, name="st", tag="st", bufs=2, align_bytes=64)
+            dst = live[("st", m)][:, :, h]
+            src = live[("h", n, 1)].rearrange("p t (i j) -> p i j t", i=TI)
+            if n in SCALE_ON_VECTOR:
+                nc.vector.tensor_scalar(out=dst, in0=src, scalar1=c1[:, 0:1], scalar2=None, op0=ALU.mult)
             else:
-                nc.vector.tensor_scalar(out=st, in0=src, scalar1=c1[:, 0:1], scalar2=None, op0=ALU.mult)
+                nc.gpsimd.tensor_scalar(out=dst, in0=src, scalar1=c1[:, 0:1], scalar2=0.0, op0=ALU.mult, op1=ALU.add)
 
-        def quant_state(n):
-            st = live[("st", n)]
-            s_c = rot.tile([P, 512], U32, name="s_c", tag="s_c", bufs=2, align_bytes=64)
-            s_s = rot.tile([P, 512], U8, name="s_s", tag="s_s", bufs=2, align_bytes=64)
-            nc.vector.quantize_mx(out=s_c.bitcast(FP8X4), scales=s_s, in_=st.rearrange("p w t -> p (w t)"))
-            live[("sc", n)] = (s_c, s_s)
+        def quant_state(o):
+            m, q = divmod(o, 2)
+            st = live[("st", m)][:, TI // 2 * q : TI // 2 * (q + 1)]
+            s_c = rot.tile([P, 512], U32, name="s_c", tag="s_c", bufs=3, align_bytes=64)
+            s_s = rot.tile([P, 512], U8, name="s_s", tag="s_s", bufs=3, align_bytes=64)
+            nc.vector.quantize_mx(out=s_c.bitcast(FP8X4), scales=s_s, in_=st.rearrange("p i h j t -> p (i h j t)"))
+            live[("sc", o)] = (s_c, s_s)
 
-        def z_matmuls(n):
-            s_c, s_s = live[("sc", n)]
+        def z_matmuls(o):
+            s_c, s_s = live[("sc", o)]
             z1 = psum.tile([P, 4, P], F32, name="z1", tag="z1", bufs=1)
             z5s = []
             for r in range(4):
-                z5 = psum.tile([P, 512], F32, name="z5", tag="z5", bufs=4)
+                if o == NT - 1 and r < 3:
+                    z5 = psum.tile([P, 512], F32, name="z5", tag="pre", bufs=3)
+                else:
+                    z5 = psum.tile([P, 512], F32, name="z5", tag="z5", bufs=4)
                 z5s.append(z5)
                 cols = slice(P * r, P * (r + 1))
                 nc.tensor.matmul_mx(
@@ -238,12 +234,12 @@ def tile_stateencoder_pa_kernel(
                     out=z1[:, r, :], lhsT=s_c[:, cols].bitcast(FP8X4), lhsT_scale=s_s[:, cols],
                     rhs=w2c[:, 512:640].bitcast(FP8X4), rhs_scale=w2s[:, 512:640], start=True, stop=True,
                 )
-            live[("z", n)] = (z1, z5s)
+            live[("z", o)] = (z1, z5s)
 
-        def add_b2(n):
-            z1, z5s = live[("z", n)]
+        def add_b2(o):
+            z1, z5s = live[("z", o)]
             zs = rot.tile([P, 4, OUT], F32, name="zs", tag="zs", bufs=3)
-            live[("zs", n)] = zs
+            live[("zs", o)] = zs
             nc.vector.tensor_tensor(
                 out=zs[:, :, 512:640], in0=z1,
                 in1=b2b[:, 512:640].unsqueeze(1).to_broadcast([P, 4, P]), op=ALU.add,
@@ -251,76 +247,110 @@ def tile_stateencoder_pa_kernel(
             for r in range(4):
                 nc.vector.tensor_tensor(out=zs[:, r, 0:512], in0=z5s[r], in1=b2b[:, 0:512], op=ALU.add)
 
-        def finish(n, r):
-            zs = live[("zs", n)]
+        def finish(o, r):
+            zs = live[("zs", o)]
             nc.scalar.activation(out=zs[:, r, :], in_=zs[:, r, :], func=ACT.Tanh)
-            row0 = 512 * n + P * r
+            row0 = 512 * o + P * r
             nc.sync.dma_start(out=out_rows[row0 : row0 + P, :], in_=zs[:, r, :])
 
-        x_chain(0)
+        x_transposes(0)
+        x_transposes(1)
+        x_codes(0, nc.vector.tensor_copy)
+        copy_x4(0, 0, 1)
+        nc.vector.tensor_tensor(out=dd, in0=mw[:, 0:1], in1=mw[:, 1:2], op=ALU.subtract)
+        build_a(0, 0, 0, 1)
+        quant_x4(0, 0, 1)
+        nc.vector.tensor_scalar(out=dd, in0=dd, scalar1=30.0, scalar2=-30.0, op0=ALU.min, op1=ALU.max)
+        build_b(0, 0)
+        regroup_w(0, 0, "V")
+        x_codes(1, nc.scalar.copy)
+        nc.scalar.activation(out=rr, in_=dd, func=ACT.Exp)
+        regroup_w(0, 1, "S")
+        quant_w(0, 0)
+        copy_x4(0, 1, 2)
+        quant_w(0, 1)
+        quant_x4(0, 1, 2)
         btp = psum.tile([P, P], BF16, name="btp", tag="pre", bufs=3)
         nc.tensor.transpose(btp, bt, ident)
         nc.vector.tensor_copy(out=bias_sb, in_=btp[:, 0:8])
-        regroup_w(0, 0, "S")
-        regroup_w(0, 1, "V")
-        build_b(0, [0])
-        quant_w(0, 0)
-        quant_w(0, 1)
-        regroup_w(0, 2, "S")
-        regroup_w(0, 3, "V")
+        regroup_w(0, 2, "V")
+        build_a(0, 1, 0, 1)
         quant_w(0, 2)
+        regroup_w(0, 3, "V")
+        copy_x4(1, 0, 2)
         quant_w(0, 3)
-        nc.vector.tensor_tensor(out=dd, in0=mw[:, 0:1], in1=mw[:, 1:2], op=ALU.subtract)
-        nc.vector.tensor_scalar(out=dd, in0=dd, scalar1=30.0, scalar2=-30.0, op0=ALU.min, op1=ALU.max)
-        x_chain(1)
-        build_b(0, [1])
+        quant_x4(1, 0, 2)
         regroup_w(1, 0, "V")
+        build_a(0, 0, 1, 2)
+        build_b(0, 1)
         quant_w(1, 0)
+        regroup_w(1, 1, "V")
+        regroup_w(1, 2, "V")
+        quant_w(1, 1)
+        regroup_w(1, 3, "V")
+        quant_w(1, 2)
+        quant_w(1, 3)
+        build_a(0, 1, 1, 2)
 
-        build_b(1, [0])
+        def hidden(n, s):
+            for t in range(4):
+                pre_act(n, s, t)
+
+        for n in range(AHEAD):
+            hidden(n, 0)
+        nc.vector.tensor_scalar(out=den, in0=rr, scalar1=1.0, scalar2=None, op0=ALU.add)
+        build_b(1, 0)
+        nc.vector.reciprocal(out=w1, in_=den)
+        build_b(1, 1)
+        nc.vector.tensor_tensor(out=c1, in0=w1, in1=gm, op=ALU.mult)
         for n in range(NT + LAG):
             if n < NT:
-                for k in range(8):
-                    s, t = divmod(k, 4)
-                    if n == 0 and k == 4:
-                        nc.scalar.activation(out=rr, in_=dd, func=ACT.Exp)
-                        regroup_w(1, 1, "S")
-                        regroup_w(1, 2, "V")
-                        quant_w(1, 1)
-                        quant_w(1, 2)
-                        regroup_w(1, 3, "V")
-                        quant_w(1, 3)
-                        build_b(1, [1])
-                        nc.vector.tensor_scalar(out=den, in0=rr, scalar1=1.0, scalar2=None, op0=ALU.add)
-                        nc.vector.reciprocal(out=w1, in_=den)
-                        nc.vector.tensor_tensor(out=c1, in0=w1, in1=gm, op=ALU.mult)
-                    pre_act(n, s, t)
-                    if s == 1:
-                        for t0, t1 in STT_PIECES:
-                            if t1 == t + 1:
-                                stt(n, t0, t1)
-            if 0 <= n - 1 < NT:
-                z_matmuls(n - 1)
-            if n < NT:
-                scale_regroup(n)
-            if 0 <= n - 1 < NT:
-                add_b2(n - 1)
+                hidden(n, 1)
+            if n == 3:
+                z_matmuls(0)
+            if 0 <= n - 1 < NT and n - 1 not in SCALE_ON_VECTOR:
+                scale_regroup(n - 1)
+            if n == NT:
+                quant_state(NT - 2)
+                quant_state(NT - 1)
+            if 0 <= n - 3 < NT:
+                add_b2(n - 3)
+            if 0 <= n - 2 < NT - 2:
+                quant_state(n - 2)
             if n == 0:
+                mix(0, 0, 4)
                 nc.vector.tensor_copy(out=w2g, in_=w2_raw.rearrange("p k n -> p n k"))
+            if n % 2 == 0 and n + 4 < NT:
+                m = n // 2 + 2
+                copy_x4(m, 0, 2)
+            if n == 0:
+                scale_regroup(0)
+            if n % 2 == 0 and n + 4 < NT:
+                quant_x4(m, 0, 2)
+            if n % 2 == 1 and n + 3 < NT:
+                m = (n + 3) // 2
+                build_b(m, 0)
+                build_b(m, 1)
+            if n in (2, 4):
+                build_a(1, n // 2 - 1, 0, 2)
+            if n == 0:
                 flat = w2g.rearrange("p n k -> p (n k)")
                 nc.vector.quantize_mx(out=w2c[:, 0:512].bitcast(FP8X4), scales=w2s[:, 0:512], in_=flat[:, 0:2048])
                 nc.vector.quantize_mx(
                     out=w2c[:, 512:640].bitcast(FP8X4), scales=w2s[:, 512:640], in_=flat[:, 2048:2560]
                 )
-            if n < NT:
-                quant_state(n)
-            if n == 1:
-                x_rest_b0(0)
-                x_rest_b0(1)
-            if n in (4, 5):
-                x_rest_b1(n - 4)
-            if n + 2 < NT:
-                build_b(n + 2, [0, 1])
+            if 0 < n < NT:
+                pieces = 4 if n == NT - 1 else 1
+                for piece in range(pieces):
+                    mix(n, 4 * piece // pieces, 4 * (piece + 1) // pieces)
+                if n in SCALE_ON_VECTOR:
+                    scale_regroup(n)
+            if n + AHEAD < NT:
+                hidden(n + AHEAD, 0)
+            if 0 < n - 2 < NT - 1:
+                z_matmuls(n - 2)
+            if n == NT:
+                z_matmuls(NT - 1)
             if n - LAG >= 0:
                 for r in range(4):
                     finish(n - LAG, r)

@@ -14,12 +14,13 @@ ALU = mybir.AluOpType
 
 P = 128
 B, L, D, H, OUT = 2, 64, 512, 512, 640
-TI, TJ = 16, 32
+TI, TJ = 16, 16
 NT = B * L * L // 512
 NM = NT // 2
 FLOPS = 4 * 2 * (B * L) * D * H + 2 * (B * L * L) * H * OUT
 SCALE_ON_VECTOR = (0, 1, NT - 1)
 LAG = 3
+X4_CHUNKS = ((0, 16), (16, 32), (32, 64), (64, 128))
 AHEAD = 2
 
 
@@ -70,9 +71,9 @@ def tile_stateencoder_pa_kernel(
         x1 = keep.tile([P, 2, P, 4], BF16, name="x1", align_bytes=64)
         xc1 = keep.tile([P, 2, P], U32, name="xc1", align_bytes=64)
         xs1 = keep.tile([P, 2, P], U8, name="xs1", align_bytes=64)
-        xs4 = keep.tile([P, NM, 2, 4 * TI], U8, name="xs4", align_bytes=64)
-        a_c = keep.tile([P, 2, B, 2, 512], U32, name="a_c", align_bytes=64)
-        a_s = keep.tile([P, 2, B, 2, 512], U8, name="a_s", align_bytes=64)
+        xs4 = keep.tile([P, 8 * P], U8, name="xs4", align_bytes=64)
+        a_c = keep.tile([P, 2, B * 4, 256], U32, name="a_c", align_bytes=64)
+        a_s = keep.tile([P, 2, B * 4, 256], U8, name="a_s", align_bytes=64)
         wc = keep.tile([P, 2, 4, 256], U32, name="wc", align_bytes=64)
         ws = keep.tile([P, 2, 4, 256], U8, name="ws", align_bytes=64)
         w2g = keep.tile([P, OUT, 4], BF16, name="w2g", align_bytes=64)
@@ -85,14 +86,14 @@ def tile_stateencoder_pa_kernel(
         w1 = keep.tile([P, 1], F32, name="w1")
         c1 = keep.tile([P, 1], F32, name="c1")
         xs1_words = xs1.rearrange("p s c -> p (s c)").bitcast(I32).rearrange("p (s w) -> p s w", s=2)
-        xs4_words = xs4.rearrange("p m s c -> p (m s c)").bitcast(I32).rearrange("p (m s k) -> p m s k", m=NM, s=2)
+        xs4_words = xs4.bitcast(I32)
         a_words = (
-            a_s.rearrange("p s b h c -> p (s b h c)").bitcast(I32)
-            .rearrange("p (s b h r w) -> p s b h r w", s=2, b=B, h=2, r=TI)
+            a_s.rearrange("p s b c -> p (s b c)").bitcast(I32)
+            .rearrange("p (s b i w) -> p s b i w", s=2, b=B * 4, i=TI)
         )
 
         nc.vector.memset(xs1.rearrange("p s c -> p (s c)").bitcast(I32), 0)
-        nc.vector.memset(xs4.rearrange("p m s c -> p (m s c)").bitcast(I32), 0)
+        nc.vector.memset(xs4_words, 0)
 
         live = {}
         w_grouped = {}
@@ -110,45 +111,58 @@ def tile_stateencoder_pa_kernel(
                 in_=x1[:, s].rearrange("p r t -> p (r t)"),
             )
 
-        def copy_x4(m, s0, s1):
-            if ("x4", m) not in live:
-                live[("x4", m)] = rot.tile([P, 2, TI, 4, 4], BF16, name="x4", tag="x4", bufs=2, align_bytes=64)
+        def copy_x4(chunk, s0, s1):
+            tok0, tok1 = X4_CHUNKS[chunk]
+            nt = tok1 - tok0
+            if ("x4", chunk) not in live:
+                live[("x4", chunk)] = rot.tile(
+                    [P, 2, nt, 4, 4], BF16, name="x4_%d" % chunk, tag="x4_%d" % chunk, bufs=1, align_bytes=64
+                )
             nc.vector.tensor_copy(
-                out=live[("x4", m)][:, s0:s1],
-                in_=x1[:, s0:s1, TI * m : TI * (m + 1), :].unsqueeze(3).to_broadcast([P, s1 - s0, TI, 4, 4]),
+                out=live[("x4", chunk)][:, s0:s1],
+                in_=x1[:, s0:s1, tok0:tok1, :].unsqueeze(3).to_broadcast([P, s1 - s0, nt, 4, 4]),
             )
 
-        def quant_x4(m, s0, s1):
-            xc4 = rot.tile([P, 2, 4 * TI], U32, name="xc4", tag="xc4", bufs=2, align_bytes=64)
+        def quant_x4(chunk, s0, s1):
+            tok0, tok1 = X4_CHUNKS[chunk]
+            nt = 4 * (tok1 - tok0)
+            xc4 = rot.tile([P, (s1 - s0) * nt], U32, name="xc4_%d" % chunk, tag="xc4_%d" % chunk, bufs=1, align_bytes=64)
             nc.vector.quantize_mx(
-                out=xc4[:, s0:s1].rearrange("p s c -> p (s c)").bitcast(FP8X4),
-                scales=xs4[:, m, s0:s1].rearrange("p s c -> p (s c)"),
-                in_=live[("x4", m)][:, s0:s1].rearrange("p s i c t -> p (s i c t)"),
+                out=xc4.bitcast(FP8X4), scales=xs4[:, 8 * tok0 + s0 * nt : 8 * tok0 + s1 * nt],
+                in_=live[("x4", chunk)][:, s0:s1].rearrange("p s i c t -> p (s i c t)"),
             )
 
-        def build_a(b, h, s0, s1):
+        def build_a(k0, k1, s0, s1):
+            ns, nk = s1 - s0, k1 - k0
+            nc.vector.tensor_copy(
+                out=a_c[:, s0:s1, k0:k1, :].bitcast(I32).rearrange("p s k (i j) -> p s k i j", i=TI),
+                in_=xc1[:, s0:s1, TJ * k0 : TJ * k1].bitcast(I32).rearrange("p s (k j) -> p s k j", j=TJ)
+                .unsqueeze(3).to_broadcast([P, ns, nk, TI, TJ]),
+            )
+            nc.vector.tensor_copy(
+                out=a_words[:, s0:s1, k0:k1],
+                in_=xs1_words[:, s0:s1, TJ // 4 * k0 : TJ // 4 * k1].rearrange("p s (k w) -> p s k w", w=TJ // 4)
+                .unsqueeze(3).to_broadcast([P, ns, nk, TI, TJ // 4]),
+            )
+
+        def build_b(m, s0, s1):
+            if ("b", m) not in live:
+                b_c = rot.tile([P, 2, 256], U32, name="b_c", tag="b_c", bufs=3, align_bytes=64)
+                b_s = rot.tile([P, 2, 256], U8, name="b_s", tag="b_s", bufs=3, align_bytes=64)
+                live[("b", m)] = (b_c, b_s)
+            b_c, b_s = live[("b", m)]
             ns = s1 - s0
-            tok0 = L * b + TJ * h
             nc.vector.tensor_copy(
-                out=a_c[:, s0:s1, b, h, :].bitcast(I32).rearrange("p s (i j) -> p s i j", i=TI),
-                in_=xc1[:, s0:s1, tok0 : tok0 + TJ].bitcast(I32).unsqueeze(2).to_broadcast([P, ns, TI, TJ]),
+                out=b_c[:, s0:s1].bitcast(I32).rearrange("p s (i j) -> p s i j", i=TI),
+                in_=xc1[:, s0:s1, TI * m : TI * (m + 1)].bitcast(I32).unsqueeze(3).to_broadcast([P, ns, TI, TJ]),
             )
+            tok0, tok1 = [c for c in X4_CHUNKS if c[0] <= TI * m < c[1]][0]
+            words = xs4_words[:, 2 * tok0 : 2 * tok1].rearrange("p (s i) -> p s i", s=2)
             nc.vector.tensor_copy(
-                out=a_words[:, s0:s1, b, h],
-                in_=xs1_words[:, s0:s1, tok0 // 4 : (tok0 + TJ) // 4].unsqueeze(2).to_broadcast([P, ns, TI, TJ // 4]),
-            )
-
-        def build_b(m, s):
-            b_c = rot.tile([P, 512], U32, name="b_c%d" % s, tag="b_c%d" % s, bufs=2, align_bytes=64)
-            b_s = rot.tile([P, 512], U8, name="b_s%d" % s, tag="b_s%d" % s, bufs=2, align_bytes=64)
-            live[("b", m, s)] = (b_c, b_s)
-            nc.vector.tensor_copy(
-                out=b_c.bitcast(I32).rearrange("p (i j) -> p i j", i=TI),
-                in_=xc1[:, s, TI * m : TI * (m + 1)].bitcast(I32).unsqueeze(2).to_broadcast([P, TI, TJ]),
-            )
-            nc.vector.tensor_copy(
-                out=b_s.bitcast(I32).rearrange("p (i w) -> p i w", i=TI),
-                in_=xs4_words[:, m, s].unsqueeze(2).to_broadcast([P, TI, TJ // 4]),
+                out=b_s.rearrange("p s c -> p (s c)").bitcast(I32)
+                .rearrange("p (s i w) -> p s i w", s=2, i=TI)[:, s0:s1],
+                in_=words[:, s0:s1, TI * m - tok0 : TI * (m + 1) - tok0].unsqueeze(3)
+                .to_broadcast([P, ns, TI, TJ // 4]),
             )
 
         def regroup_w(s, c, engine):
@@ -169,25 +183,28 @@ def tile_stateencoder_pa_kernel(
         def pre_act(n, s, t):
             m, h = divmod(n, 2)
             b = m // (NM // B)
-            b_c, b_s = live[("b", m, s)]
+            b_c, b_s = live[("b", m)]
             if ("h", n, s) not in live:
                 live[("h", n, s)] = rot.tile([P, 4, 512], F32, name="hs%d" % s, tag="hs%d" % s, bufs=(AHEAD + 2, 3)[s])
             hs = live[("h", n, s)]
-            pre = psum.tile([P, 512], F32, name="pre", tag="pre", bufs=3)
-            nc.tensor.matmul_mx(
-                out=pre,
-                lhsT=wc[:, s, t, 0:P].bitcast(FP8X4), lhsT_scale=ws[:, s, t, 0:P],
-                rhs=a_c[:, s, b, h, :].bitcast(FP8X4), rhs_scale=a_s[:, s, b, h, :],
-                start=True, stop=False,
-            )
-            nc.tensor.matmul_mx(
-                out=pre,
-                lhsT=wc[:, s, t, P : 2 * P].bitcast(FP8X4), lhsT_scale=ws[:, s, t, P : 2 * P],
-                rhs=b_c.bitcast(FP8X4), rhs_scale=b_s,
-                start=False, stop=True,
-            )
+            pre = psum.tile([P, 2, 256], F32, name="pre", tag="pre", bufs=3)
+            for g in range(2):
+                k = 4 * b + 2 * h + g
+                nc.tensor.matmul_mx(
+                    out=pre[:, g],
+                    lhsT=wc[:, s, t, 0:P].bitcast(FP8X4), lhsT_scale=ws[:, s, t, 0:P],
+                    rhs=a_c[:, s, k].bitcast(FP8X4), rhs_scale=a_s[:, s, k],
+                    start=True, stop=False,
+                )
+                nc.tensor.matmul_mx(
+                    out=pre[:, g],
+                    lhsT=wc[:, s, t, P : 2 * P].bitcast(FP8X4), lhsT_scale=ws[:, s, t, P : 2 * P],
+                    rhs=b_c[:, s].bitcast(FP8X4), rhs_scale=b_s[:, s],
+                    start=False, stop=True,
+                )
             nc.scalar.activation(
-                out=hs[:, t, :], in_=pre, func=ACT.Tanh,
+                out=hs[:, t, :].rearrange("p (i g j) -> p g i j", i=TI, g=2),
+                in_=pre.rearrange("p g (i j) -> p g i j", i=TI), func=ACT.Tanh,
                 bias=bias_sb[:, 4 * s + t : 4 * s + t + 1], scale=1.0,
             )
 
@@ -199,7 +216,7 @@ def tile_stateencoder_pa_kernel(
         def scale_regroup(n):
             m, h = divmod(n, 2)
             if h == 0:
-                live[("st", m)] = rot.tile([P, TI, 2, TJ, 4], BF16, name="st", tag="st", bufs=2, align_bytes=64)
+                live[("st", m)] = rot.tile([P, TI, 2, 2 * TJ, 4], BF16, name="st", tag="st", bufs=2, align_bytes=64)
             dst = live[("st", m)][:, :, h]
             src = live[("h", n, 1)].rearrange("p t (i j) -> p i j t", i=TI)
             if n in SCALE_ON_VECTOR:
@@ -207,20 +224,28 @@ def tile_stateencoder_pa_kernel(
             else:
                 nc.gpsimd.tensor_scalar(out=dst, in0=src, scalar1=c1[:, 0:1], scalar2=0.0, op0=ALU.mult, op1=ALU.add)
 
-        def quant_state(o):
-            m, q = divmod(o, 2)
-            st = live[("st", m)][:, TI // 2 * q : TI // 2 * (q + 1)]
-            s_c = rot.tile([P, 512], U32, name="s_c", tag="s_c", bufs=3, align_bytes=64)
-            s_s = rot.tile([P, 512], U8, name="s_s", tag="s_s", bufs=3, align_bytes=64)
+        def quant_state(m, q0, q1):
+            st = live[("st", m)][:, TI // 2 * q0 : TI // 2 * q1]
+            cols = 512 * (q1 - q0)
+            s_c = rot.tile([P, cols], U32, name="s_c%d" % (q1 - q0), tag="s_c%d" % (q1 - q0), bufs=2, align_bytes=64)
+            s_s = rot.tile([P, cols], U8, name="s_s%d" % (q1 - q0), tag="s_s%d" % (q1 - q0), bufs=2, align_bytes=64)
             nc.vector.quantize_mx(out=s_c.bitcast(FP8X4), scales=s_s, in_=st.rearrange("p i h j t -> p (i h j t)"))
-            live[("sc", o)] = (s_c, s_s)
+            for q in range(q0, q1):
+                cols = slice(512 * (q - q0), 512 * (q - q0 + 1))
+                live[("sc", 2 * m + q)] = (s_c[:, cols], s_s[:, cols])
 
         def z_matmuls(o):
             s_c, s_s = live[("sc", o)]
             z1 = psum.tile([P, 4, P], F32, name="z1", tag="z1", bufs=1)
             z5s = []
             for r in range(4):
-                if o == NT - 1 and r < 3:
+                cols = slice(P * r, P * (r + 1))
+                nc.tensor.matmul_mx(
+                    out=z1[:, r, :], lhsT=s_c[:, cols].bitcast(FP8X4), lhsT_scale=s_s[:, cols],
+                    rhs=w2c[:, 512:640].bitcast(FP8X4), rhs_scale=w2s[:, 512:640], start=True, stop=True,
+                )
+            for r in range(4):
+                if o == NT - 2 and r < 3:
                     z5 = psum.tile([P, 512], F32, name="z5", tag="pre", bufs=3)
                 else:
                     z5 = psum.tile([P, 512], F32, name="z5", tag="z5", bufs=4)
@@ -229,10 +254,6 @@ def tile_stateencoder_pa_kernel(
                 nc.tensor.matmul_mx(
                     out=z5, lhsT=s_c[:, cols].bitcast(FP8X4), lhsT_scale=s_s[:, cols],
                     rhs=w2c[:, 0:512].bitcast(FP8X4), rhs_scale=w2s[:, 0:512], start=True, stop=True,
-                )
-                nc.tensor.matmul_mx(
-                    out=z1[:, r, :], lhsT=s_c[:, cols].bitcast(FP8X4), lhsT_scale=s_s[:, cols],
-                    rhs=w2c[:, 512:640].bitcast(FP8X4), rhs_scale=w2s[:, 512:640], start=True, stop=True,
                 )
             live[("z", o)] = (z1, z5s)
 
@@ -247,24 +268,23 @@ def tile_stateencoder_pa_kernel(
             for r in range(4):
                 nc.vector.tensor_tensor(out=zs[:, r, 0:512], in0=z5s[r], in1=b2b[:, 0:512], op=ALU.add)
 
-        def finish(o, r):
+        def finish(o, r0, r1):
             zs = live[("zs", o)]
-            nc.scalar.activation(out=zs[:, r, :], in_=zs[:, r, :], func=ACT.Tanh)
-            row0 = 512 * o + P * r
-            nc.sync.dma_start(out=out_rows[row0 : row0 + P, :], in_=zs[:, r, :])
+            flat = zs[:, r0:r1].rearrange("p r o -> p (r o)")
+            nc.scalar.activation(out=flat, in_=flat, func=ACT.Tanh)
+            for r in range(r0, r1):
+                row0 = 512 * o + P * r
+                nc.sync.dma_start(out=out_rows[row0 : row0 + P, :], in_=zs[:, r, :])
 
         x_transposes(0)
         x_transposes(1)
         x_codes(0, nc.vector.tensor_copy)
         copy_x4(0, 0, 1)
-        nc.vector.tensor_tensor(out=dd, in0=mw[:, 0:1], in1=mw[:, 1:2], op=ALU.subtract)
-        build_a(0, 0, 0, 1)
+        build_a(0, 2, 0, 1)
         quant_x4(0, 0, 1)
-        nc.vector.tensor_scalar(out=dd, in0=dd, scalar1=30.0, scalar2=-30.0, op0=ALU.min, op1=ALU.max)
-        build_b(0, 0)
+        build_b(0, 0, 1)
         regroup_w(0, 0, "V")
         x_codes(1, nc.scalar.copy)
-        nc.scalar.activation(out=rr, in_=dd, func=ACT.Exp)
         regroup_w(0, 1, "S")
         quant_w(0, 0)
         copy_x4(0, 1, 2)
@@ -273,24 +293,26 @@ def tile_stateencoder_pa_kernel(
         btp = psum.tile([P, P], BF16, name="btp", tag="pre", bufs=3)
         nc.tensor.transpose(btp, bt, ident)
         nc.vector.tensor_copy(out=bias_sb, in_=btp[:, 0:8])
-        regroup_w(0, 2, "V")
-        build_a(0, 1, 0, 1)
-        quant_w(0, 2)
+        regroup_w(0, 2, "S")
         regroup_w(0, 3, "V")
-        copy_x4(1, 0, 2)
+        quant_w(0, 2)
         quant_w(0, 3)
-        quant_x4(1, 0, 2)
+        build_a(2, 4, 0, 1)
         regroup_w(1, 0, "V")
-        build_a(0, 0, 1, 2)
-        build_b(0, 1)
+        build_a(0, 4, 1, 2)
         quant_w(1, 0)
+        build_b(0, 1, 2)
         regroup_w(1, 1, "V")
-        regroup_w(1, 2, "V")
+        copy_x4(1, 0, 2)
         quant_w(1, 1)
-        regroup_w(1, 3, "V")
+        regroup_w(1, 2, "V")
+        quant_x4(1, 0, 2)
         quant_w(1, 2)
+        regroup_w(1, 3, "V")
+        nc.vector.tensor_tensor(out=dd, in0=mw[:, 0:1], in1=mw[:, 1:2], op=ALU.subtract)
         quant_w(1, 3)
-        build_a(0, 1, 1, 2)
+        nc.vector.tensor_scalar(out=dd, in0=dd, scalar1=30.0, scalar2=-30.0, op0=ALU.min, op1=ALU.max)
+        build_b(1, 0, 2)
 
         def hidden(n, s):
             for t in range(4):
@@ -298,11 +320,6 @@ def tile_stateencoder_pa_kernel(
 
         for n in range(AHEAD):
             hidden(n, 0)
-        nc.vector.tensor_scalar(out=den, in0=rr, scalar1=1.0, scalar2=None, op0=ALU.add)
-        build_b(1, 0)
-        nc.vector.reciprocal(out=w1, in_=den)
-        build_b(1, 1)
-        nc.vector.tensor_tensor(out=c1, in0=w1, in1=gm, op=ALU.mult)
         for n in range(NT + LAG):
             if n < NT:
                 hidden(n, 1)
@@ -311,34 +328,34 @@ def tile_stateencoder_pa_kernel(
             if 0 <= n - 1 < NT and n - 1 not in SCALE_ON_VECTOR:
                 scale_regroup(n - 1)
             if n == NT:
-                quant_state(NT - 2)
-                quant_state(NT - 1)
+                quant_state(NM - 1, 0, 1)
+                quant_state(NM - 1, 1, 2)
             if 0 <= n - 3 < NT:
                 add_b2(n - 3)
-            if 0 <= n - 2 < NT - 2:
-                quant_state(n - 2)
+            if n % 2 == 0 and 2 <= n < NT:
+                quant_state(n // 2 - 1, 0, 2)
             if n == 0:
+                nc.scalar.activation(out=rr, in_=dd, func=ACT.Exp)
                 mix(0, 0, 4)
+                nc.vector.tensor_scalar(out=den, in0=rr, scalar1=1.0, scalar2=None, op0=ALU.add)
                 nc.vector.tensor_copy(out=w2g, in_=w2_raw.rearrange("p k n -> p n k"))
-            if n % 2 == 0 and n + 4 < NT:
-                m = n // 2 + 2
-                copy_x4(m, 0, 2)
-            if n == 0:
-                scale_regroup(0)
-            if n % 2 == 0 and n + 4 < NT:
-                quant_x4(m, 0, 2)
-            if n % 2 == 1 and n + 3 < NT:
-                m = (n + 3) // 2
-                build_b(m, 0)
-                build_b(m, 1)
-            if n in (2, 4):
-                build_a(1, n // 2 - 1, 0, 2)
-            if n == 0:
+                nc.vector.reciprocal(out=w1, in_=den)
+                copy_x4(2, 0, 2)
+                nc.vector.tensor_tensor(out=c1, in0=w1, in1=gm, op=ALU.mult)
                 flat = w2g.rearrange("p n k -> p (n k)")
                 nc.vector.quantize_mx(out=w2c[:, 0:512].bitcast(FP8X4), scales=w2s[:, 0:512], in_=flat[:, 0:2048])
+                scale_regroup(0)
                 nc.vector.quantize_mx(
                     out=w2c[:, 512:640].bitcast(FP8X4), scales=w2s[:, 512:640], in_=flat[:, 2048:2560]
                 )
+                quant_x4(2, 0, 2)
+            if n == 4:
+                copy_x4(3, 0, 2)
+                quant_x4(3, 0, 2)
+            if n == 5:
+                build_a(4, 8, 0, 2)
+            if n % 2 == 1 and n + 3 < NT:
+                build_b((n + 3) // 2, 0, 2)
             if 0 < n < NT:
                 pieces = 4 if n == NT - 1 else 1
                 for piece in range(pieces):
@@ -352,5 +369,6 @@ def tile_stateencoder_pa_kernel(
             if n == NT:
                 z_matmuls(NT - 1)
             if n - LAG >= 0:
-                for r in range(4):
-                    finish(n - LAG, r)
+                pieces = 4 if n - LAG >= NT - 3 else 2
+                for piece in range(pieces):
+                    finish(n - LAG, 4 * piece // pieces, 4 * (piece + 1) // pieces)

@@ -18,7 +18,7 @@ TI, TJ = 16, 16
 NT = B * L * L // 512
 NM = NT // 2
 FLOPS = 4 * 2 * (B * L) * D * H + 2 * (B * L * L) * H * OUT
-SCALE_ON_VECTOR = (0, 1, NT - 1)
+SCALE_ON_VECTOR = (0, 1)
 LAG = 3
 X4_CHUNKS = ((0, 16), (16, 32), (32, 64), (64, 128))
 AHEAD = 2
@@ -167,11 +167,14 @@ def tile_stateencoder_pa_kernel(
 
         def regroup_w(s, c, engine):
             wg = rot.tile([P, 2, P, 4], BF16, name="wg", tag="wg", bufs=4, align_bytes=64)
-            src = w_raw[s][:, :, P * c : P * (c + 1)].rearrange("p (g k) m -> p g m k", g=2)
+            src = w_raw[s][:, :, P * c : P * (c + 1)]
             if engine == "V":
-                nc.vector.tensor_copy(out=wg, in_=src)
+                nc.vector.tensor_copy(
+                    out=wg.rearrange("p g (c i) k -> p g c k i", i=4),
+                    in_=src.rearrange("p (g k) (c i) -> p g c k i", g=2, i=4),
+                )
             else:
-                nc.scalar.copy(out=wg, in_=src)
+                nc.scalar.copy(out=wg, in_=src.rearrange("p (g k) m -> p g m k", g=2))
             w_grouped[(s, c)] = wg
 
         def quant_w(s, c):
@@ -321,24 +324,31 @@ def tile_stateencoder_pa_kernel(
         for n in range(AHEAD):
             hidden(n, 0)
         for n in range(NT + LAG):
-            if n < NT:
+            if n < NT - 1:
                 hidden(n, 1)
+            if n == NT - 2:
+                hidden(NT - 1, 1)
             if n == 3:
                 z_matmuls(0)
-            if 0 <= n - 1 < NT and n - 1 not in SCALE_ON_VECTOR:
+            if 0 <= n - 1 < NT - 1 and n - 1 not in SCALE_ON_VECTOR:
                 scale_regroup(n - 1)
+            if n == NT - 1:
+                scale_regroup(NT - 1)
+            if 0 <= n - 3 < NT:
+                add_b2(n - 3)
             if n == NT:
                 quant_state(NM - 1, 0, 1)
                 quant_state(NM - 1, 1, 2)
-            if 0 <= n - 3 < NT:
-                add_b2(n - 3)
             if n % 2 == 0 and 2 <= n < NT:
                 quant_state(n // 2 - 1, 0, 2)
             if n == 0:
                 nc.scalar.activation(out=rr, in_=dd, func=ACT.Exp)
                 mix(0, 0, 4)
                 nc.vector.tensor_scalar(out=den, in0=rr, scalar1=1.0, scalar2=None, op0=ALU.add)
-                nc.vector.tensor_copy(out=w2g, in_=w2_raw.rearrange("p k n -> p n k"))
+                nc.vector.tensor_copy(
+                    out=w2g.rearrange("p (c i) k -> p c k i", i=4),
+                    in_=w2_raw.rearrange("p k (c i) -> p c k i", i=4),
+                )
                 nc.vector.reciprocal(out=w1, in_=den)
                 copy_x4(2, 0, 2)
                 nc.vector.tensor_tensor(out=c1, in0=w1, in1=gm, op=ALU.mult)
@@ -356,17 +366,17 @@ def tile_stateencoder_pa_kernel(
                 build_a(4, 8, 0, 2)
             if n % 2 == 1 and n + 3 < NT:
                 build_b((n + 3) // 2, 0, 2)
-            if 0 < n < NT:
-                pieces = 4 if n == NT - 1 else 1
-                for piece in range(pieces):
-                    mix(n, 4 * piece // pieces, 4 * (piece + 1) // pieces)
+            if 0 < n < NT - 1:
+                mix(n, 0, 4)
+                if n == NT - 2:
+                    mix(NT - 1, 0, 4)
                 if n in SCALE_ON_VECTOR:
                     scale_regroup(n)
             if n + AHEAD < NT:
                 hidden(n + AHEAD, 0)
             if 0 < n - 2 < NT - 1:
                 z_matmuls(n - 2)
-            if n == NT:
+            if n == NT + 1:
                 z_matmuls(NT - 1)
             if n - LAG >= 0:
                 pieces = 4 if n - LAG >= NT - 3 else 2

@@ -21,6 +21,7 @@ FLOPS = 4 * 2 * (B * L) * D * H + 2 * (B * L * L) * H * OUT
 SCALE_ON_VECTOR = (0, 1)
 LAG = 3
 X4_CHUNKS = ((0, 16), (16, 32), (32, 64), (64, 128))
+TURN = 5
 AHEAD = 2
 
 
@@ -92,6 +93,8 @@ def tile_stateencoder_pa_kernel(
             .rearrange("p (s b i w) -> p s b i w", s=2, b=B * 4, i=TI)
         )
 
+        warm = keep.tile([P, 512], BF16, name="warm")
+        nc.vector.memset(warm, 0.0)
         nc.vector.memset(xs1.rearrange("p s c -> p (s c)").bitcast(I32), 0)
         nc.vector.memset(xs4_words, 0)
 
@@ -211,9 +214,9 @@ def tile_stateencoder_pa_kernel(
                 bias=bias_sb[:, 4 * s + t : 4 * s + t + 1], scale=1.0,
             )
 
-        def mix(n, t0, t1):
-            hu = live[("h", n, 0)][:, t0:t1].rearrange("p t w -> p (t w)")
-            hp = live[("h", n, 1)][:, t0:t1].rearrange("p t w -> p (t w)")
+        def mix(n):
+            hu = live[("h", n, 0)].rearrange("p t w -> p (t w)")
+            hp = live[("h", n, 1)].rearrange("p t w -> p (t w)")
             nc.vector.scalar_tensor_tensor(out=hp, in0=hu, scalar=rr[:, 0:1], in1=hp, op0=ALU.mult, op1=ALU.add)
 
         def scale_regroup(n):
@@ -279,6 +282,15 @@ def tile_stateencoder_pa_kernel(
                 row0 = 512 * o + P * r
                 nc.sync.dma_start(out=out_rows[row0 : row0 + P, :], in_=zs[:, r, :])
 
+        nc.gpsimd.tensor_tensor(out=dd, in0=mw[:, 0:1], in1=mw[:, 1:2], op=ALU.subtract)
+        nc.gpsimd.tensor_scalar(out=dd, in0=dd, scalar1=30.0, scalar2=-30.0, op0=ALU.min, op1=ALU.max)
+        warm_ps = psum.tile([P, 512], F32, name="warm_ps", tag="z5", bufs=4)
+
+        def warm_up(passes):
+            for step in range(passes):
+                nc.tensor.matmul(warm_ps, lhsT=warm[:, 0:P], rhs=warm, start=True, stop=True)
+
+        warm_up(4)
         x_transposes(0)
         x_transposes(1)
         x_codes(0, nc.vector.tensor_copy)
@@ -295,7 +307,8 @@ def tile_stateencoder_pa_kernel(
         quant_x4(0, 1, 2)
         btp = psum.tile([P, P], BF16, name="btp", tag="pre", bufs=3)
         nc.tensor.transpose(btp, bt, ident)
-        nc.vector.tensor_copy(out=bias_sb, in_=btp[:, 0:8])
+        warm_up(4)
+        nc.scalar.copy(out=bias_sb, in_=btp[:, 0:8])
         regroup_w(0, 2, "S")
         regroup_w(0, 3, "V")
         quant_w(0, 2)
@@ -312,28 +325,35 @@ def tile_stateencoder_pa_kernel(
         quant_x4(1, 0, 2)
         quant_w(1, 2)
         regroup_w(1, 3, "V")
-        nc.vector.tensor_tensor(out=dd, in0=mw[:, 0:1], in1=mw[:, 1:2], op=ALU.subtract)
         quant_w(1, 3)
-        nc.vector.tensor_scalar(out=dd, in0=dd, scalar1=30.0, scalar2=-30.0, op0=ALU.min, op1=ALU.max)
         build_b(1, 0, 2)
+        nc.vector.tensor_copy(
+            out=w2g.rearrange("p (c i) k -> p c k i", i=4),
+            in_=w2_raw.rearrange("p k (c i) -> p c k i", i=4),
+        )
 
         def hidden(n, s):
             for t in range(4):
                 pre_act(n, s, t)
 
-        for n in range(AHEAD):
-            hidden(n, 0)
+        hidden(0, 0)
+        nc.scalar.activation(out=rr, in_=dd, func=ACT.Exp)
+        nc.gpsimd.tensor_scalar(out=den, in0=rr, scalar1=1.0, scalar2=0.0, op0=ALU.add, op1=ALU.add)
+        nc.vector.reciprocal(out=w1, in_=den)
+        nc.gpsimd.tensor_tensor(out=c1, in0=w1, in1=gm, op=ALU.mult)
+        hidden(1, 0)
         for n in range(NT + LAG):
-            if n < NT - 1:
+            if n <= TURN:
                 hidden(n, 1)
-            if n == NT - 2:
-                hidden(NT - 1, 1)
+            if n == TURN:
+                hidden(n + 1, 1)
+            if TURN < n < NT - 1:
+                hidden(n + 1, 0)
+                hidden(n + 1, 1)
             if n == 3:
                 z_matmuls(0)
-            if 0 <= n - 1 < NT - 1 and n - 1 not in SCALE_ON_VECTOR:
+            if 0 <= n - 1 < NT and n - 1 not in SCALE_ON_VECTOR:
                 scale_regroup(n - 1)
-            if n == NT - 1:
-                scale_regroup(NT - 1)
             if 0 <= n - 3 < NT:
                 add_b2(n - 3)
             if n == NT:
@@ -342,16 +362,8 @@ def tile_stateencoder_pa_kernel(
             if n % 2 == 0 and 2 <= n < NT:
                 quant_state(n // 2 - 1, 0, 2)
             if n == 0:
-                nc.scalar.activation(out=rr, in_=dd, func=ACT.Exp)
-                mix(0, 0, 4)
-                nc.vector.tensor_scalar(out=den, in0=rr, scalar1=1.0, scalar2=None, op0=ALU.add)
-                nc.vector.tensor_copy(
-                    out=w2g.rearrange("p (c i) k -> p c k i", i=4),
-                    in_=w2_raw.rearrange("p k (c i) -> p c k i", i=4),
-                )
-                nc.vector.reciprocal(out=w1, in_=den)
+                mix(0)
                 copy_x4(2, 0, 2)
-                nc.vector.tensor_tensor(out=c1, in0=w1, in1=gm, op=ALU.mult)
                 flat = w2g.rearrange("p n k -> p (n k)")
                 nc.vector.quantize_mx(out=w2c[:, 0:512].bitcast(FP8X4), scales=w2s[:, 0:512], in_=flat[:, 0:2048])
                 scale_regroup(0)
@@ -366,13 +378,11 @@ def tile_stateencoder_pa_kernel(
                 build_a(4, 8, 0, 2)
             if n % 2 == 1 and n + 3 < NT:
                 build_b((n + 3) // 2, 0, 2)
-            if 0 < n < NT - 1:
-                mix(n, 0, 4)
-                if n == NT - 2:
-                    mix(NT - 1, 0, 4)
+            if 0 < n < NT:
+                mix(n)
                 if n in SCALE_ON_VECTOR:
                     scale_regroup(n)
-            if n + AHEAD < NT:
+            if n < TURN:
                 hidden(n + AHEAD, 0)
             if 0 < n - 2 < NT - 1:
                 z_matmuls(n - 2)

@@ -22,7 +22,9 @@ SCALE_ON_VECTOR = (0, 1)
 LAG = 3
 X4_CHUNKS = ((0, 16), (16, 32), (32, 64), (64, 128))
 TURN = 5
-AHEAD = 2
+Z_FIRST = 3
+Z_EARLY = 9
+AHEAD = 3
 
 
 def tile_stateencoder_pa_kernel(
@@ -282,6 +284,10 @@ def tile_stateencoder_pa_kernel(
                 row0 = 512 * o + P * r
                 nc.sync.dma_start(out=out_rows[row0 : row0 + P, :], in_=zs[:, r, :])
 
+        def hidden(n, s):
+            for t in range(4):
+                pre_act(n, s, t)
+
         nc.gpsimd.tensor_tensor(out=dd, in0=mw[:, 0:1], in1=mw[:, 1:2], op=ALU.subtract)
         nc.gpsimd.tensor_scalar(out=dd, in0=dd, scalar1=30.0, scalar2=-30.0, op0=ALU.min, op1=ALU.max)
         warm_ps = psum.tile([P, 512], F32, name="warm_ps", tag="z5", bufs=4)
@@ -314,41 +320,36 @@ def tile_stateencoder_pa_kernel(
         quant_w(0, 2)
         quant_w(0, 3)
         build_a(2, 4, 0, 1)
+        hidden(0, 0)
+        nc.scalar.activation(out=rr, in_=dd, func=ACT.Exp)
+        nc.gpsimd.tensor_scalar(out=den, in0=rr, scalar1=1.0, scalar2=0.0, op0=ALU.add, op1=ALU.add)
         regroup_w(1, 0, "V")
-        build_a(0, 4, 1, 2)
+        copy_x4(1, 0, 2)
+        build_a(0, 2, 1, 2)
+        quant_x4(1, 0, 2)
         quant_w(1, 0)
         build_b(0, 1, 2)
-        regroup_w(1, 1, "V")
-        copy_x4(1, 0, 2)
-        quant_w(1, 1)
-        regroup_w(1, 2, "V")
-        quant_x4(1, 0, 2)
-        quant_w(1, 2)
-        regroup_w(1, 3, "V")
-        quant_w(1, 3)
         build_b(1, 0, 2)
+        regroup_w(1, 1, "V")
+        hidden(1, 0)
+        regroup_w(1, 2, "V")
+        hidden(2, 0)
+        quant_w(1, 1)
+        regroup_w(1, 3, "V")
+        quant_w(1, 2)
+        nc.vector.reciprocal(out=w1, in_=den)
+        nc.gpsimd.tensor_tensor(out=c1, in0=w1, in1=gm, op=ALU.mult)
+        quant_w(1, 3)
+        build_a(2, 4, 1, 2)
         nc.vector.tensor_copy(
             out=w2g.rearrange("p (c i) k -> p c k i", i=4),
             in_=w2_raw.rearrange("p k (c i) -> p c k i", i=4),
         )
 
-        def hidden(n, s):
-            for t in range(4):
-                pre_act(n, s, t)
-
-        hidden(0, 0)
-        nc.scalar.activation(out=rr, in_=dd, func=ACT.Exp)
-        nc.gpsimd.tensor_scalar(out=den, in0=rr, scalar1=1.0, scalar2=0.0, op0=ALU.add, op1=ALU.add)
-        nc.vector.reciprocal(out=w1, in_=den)
-        nc.gpsimd.tensor_tensor(out=c1, in0=w1, in1=gm, op=ALU.mult)
-        hidden(1, 0)
         for n in range(NT + LAG):
             if n <= TURN:
                 hidden(n, 1)
             if n == TURN:
-                hidden(n + 1, 1)
-            if TURN < n < NT - 1:
-                hidden(n + 1, 0)
                 hidden(n + 1, 1)
             if n == 3:
                 z_matmuls(0)
@@ -362,30 +363,43 @@ def tile_stateencoder_pa_kernel(
             if n % 2 == 0 and 2 <= n < NT:
                 quant_state(n // 2 - 1, 0, 2)
             if n == 0:
-                mix(0)
                 copy_x4(2, 0, 2)
+                mix(0)
+                quant_x4(2, 0, 2)
+                build_b(2, 0, 2)
                 flat = w2g.rearrange("p n k -> p (n k)")
-                nc.vector.quantize_mx(out=w2c[:, 0:512].bitcast(FP8X4), scales=w2s[:, 0:512], in_=flat[:, 0:2048])
                 scale_regroup(0)
+                nc.vector.quantize_mx(out=w2c[:, 0:512].bitcast(FP8X4), scales=w2s[:, 0:512], in_=flat[:, 0:2048])
                 nc.vector.quantize_mx(
                     out=w2c[:, 512:640].bitcast(FP8X4), scales=w2s[:, 512:640], in_=flat[:, 2048:2560]
                 )
-                quant_x4(2, 0, 2)
             if n == 4:
                 copy_x4(3, 0, 2)
                 quant_x4(3, 0, 2)
-            if n == 5:
+            if n == 3:
                 build_a(4, 8, 0, 2)
-            if n % 2 == 1 and n + 3 < NT:
-                build_b((n + 3) // 2, 0, 2)
+            if n % 2 == 0 and 0 < n and n // 2 + 2 < NM:
+                build_b(n // 2 + 2, 0, 2)
             if 0 < n < NT:
                 mix(n)
                 if n in SCALE_ON_VECTOR:
                     scale_regroup(n)
             if n < TURN:
                 hidden(n + AHEAD, 0)
-            if 0 < n - 2 < NT - 1:
-                z_matmuls(n - 2)
+            if n <= TURN:
+                if n > 2:
+                    z_matmuls(n - 2)
+            else:
+                ahead = [(n + 1, 1, t) for t in range(4)] if n + 1 < NT else []
+                if n + AHEAD - 1 < NT:
+                    ahead = ahead + [(n + AHEAD - 1, 0, t) for t in range(4)]
+                pos = min(len(ahead), Z_FIRST if n >= Z_EARLY else 8)
+                for args in ahead[:pos]:
+                    pre_act(args[0], args[1], args[2])
+                if n - 2 < NT - 1:
+                    z_matmuls(n - 2)
+                for args in ahead[pos:]:
+                    pre_act(args[0], args[1], args[2])
             if n == NT + 1:
                 z_matmuls(NT - 1)
             if n - LAG >= 0:

@@ -14,7 +14,7 @@ ALU = mybir.AluOpType
 
 P = 128
 B, L, D, H, OUT = 2, 64, 512, 512, 640
-TI, TJ = 16, 16
+TI, TJ = 16, 32
 NT = B * L * L // 512
 NM = NT // 2
 FLOPS = 4 * 2 * (B * L) * D * H + 2 * (B * L * L) * H * OUT
@@ -23,7 +23,7 @@ LAG = 3
 X4_CHUNKS = ((0, 16), (16, 32), (32, 64), (64, 128))
 TURN = 5
 Z_FIRST = 3
-Z_EARLY = 9
+Z_EARLY = 11
 AHEAD = 3
 
 
@@ -75,8 +75,8 @@ def tile_stateencoder_pa_kernel(
         xc1 = keep.tile([P, 2, P], U32, name="xc1", align_bytes=64)
         xs1 = keep.tile([P, 2, P], U8, name="xs1", align_bytes=64)
         xs4 = keep.tile([P, 8 * P], U8, name="xs4", align_bytes=64)
-        a_c = keep.tile([P, 2, B * 4, 256], U32, name="a_c", align_bytes=64)
-        a_s = keep.tile([P, 2, B * 4, 256], U8, name="a_s", align_bytes=64)
+        a_c = keep.tile([P, 2, B * 2, 512], U32, name="a_c", align_bytes=64)
+        a_s = keep.tile([P, 2, B * 2, 512], U8, name="a_s", align_bytes=64)
         wc = keep.tile([P, 2, 4, 256], U32, name="wc", align_bytes=64)
         ws = keep.tile([P, 2, 4, 256], U8, name="ws", align_bytes=64)
         w2g = keep.tile([P, OUT, 4], BF16, name="w2g", align_bytes=64)
@@ -92,7 +92,7 @@ def tile_stateencoder_pa_kernel(
         xs4_words = xs4.bitcast(I32)
         a_words = (
             a_s.rearrange("p s b c -> p (s b c)").bitcast(I32)
-            .rearrange("p (s b i w) -> p s b i w", s=2, b=B * 4, i=TI)
+            .rearrange("p (s b i w) -> p s b i w", s=2, b=B * 2, i=TI)
         )
 
         warm = keep.tile([P, 512], BF16, name="warm")
@@ -152,8 +152,8 @@ def tile_stateencoder_pa_kernel(
 
         def build_b(m, s0, s1):
             if ("b", m) not in live:
-                b_c = rot.tile([P, 2, 256], U32, name="b_c", tag="b_c", bufs=3, align_bytes=64)
-                b_s = rot.tile([P, 2, 256], U8, name="b_s", tag="b_s", bufs=3, align_bytes=64)
+                b_c = rot.tile([P, 2, 512], U32, name="b_c", tag="b_c", bufs=3, align_bytes=64)
+                b_s = rot.tile([P, 2, 512], U8, name="b_s", tag="b_s", bufs=3, align_bytes=64)
                 live[("b", m)] = (b_c, b_s)
             b_c, b_s = live[("b", m)]
             ns = s1 - s0
@@ -195,24 +195,22 @@ def tile_stateencoder_pa_kernel(
             if ("h", n, s) not in live:
                 live[("h", n, s)] = rot.tile([P, 4, 512], F32, name="hs%d" % s, tag="hs%d" % s, bufs=(AHEAD + 2, 3)[s])
             hs = live[("h", n, s)]
-            pre = psum.tile([P, 2, 256], F32, name="pre", tag="pre", bufs=3)
-            for g in range(2):
-                k = 4 * b + 2 * h + g
-                nc.tensor.matmul_mx(
-                    out=pre[:, g],
-                    lhsT=wc[:, s, t, 0:P].bitcast(FP8X4), lhsT_scale=ws[:, s, t, 0:P],
-                    rhs=a_c[:, s, k].bitcast(FP8X4), rhs_scale=a_s[:, s, k],
-                    start=True, stop=False,
-                )
-                nc.tensor.matmul_mx(
-                    out=pre[:, g],
-                    lhsT=wc[:, s, t, P : 2 * P].bitcast(FP8X4), lhsT_scale=ws[:, s, t, P : 2 * P],
-                    rhs=b_c[:, s].bitcast(FP8X4), rhs_scale=b_s[:, s],
-                    start=False, stop=True,
-                )
+            pre = psum.tile([P, 512], F32, name="pre", tag="pre", bufs=3)
+            k = 2 * b + h
+            nc.tensor.matmul_mx(
+                out=pre,
+                lhsT=wc[:, s, t, 0:P].bitcast(FP8X4), lhsT_scale=ws[:, s, t, 0:P],
+                rhs=a_c[:, s, k].bitcast(FP8X4), rhs_scale=a_s[:, s, k],
+                start=True, stop=False,
+            )
+            nc.tensor.matmul_mx(
+                out=pre,
+                lhsT=wc[:, s, t, P : 2 * P].bitcast(FP8X4), lhsT_scale=ws[:, s, t, P : 2 * P],
+                rhs=b_c[:, s].bitcast(FP8X4), rhs_scale=b_s[:, s],
+                start=False, stop=True,
+            )
             nc.scalar.activation(
-                out=hs[:, t, :].rearrange("p (i g j) -> p g i j", i=TI, g=2),
-                in_=pre.rearrange("p g (i j) -> p g i j", i=TI), func=ACT.Tanh,
+                out=hs[:, t, :], in_=pre, func=ACT.Tanh,
                 bias=bias_sb[:, 4 * s + t : 4 * s + t + 1], scale=1.0,
             )
 
@@ -224,7 +222,7 @@ def tile_stateencoder_pa_kernel(
         def scale_regroup(n):
             m, h = divmod(n, 2)
             if h == 0:
-                live[("st", m)] = rot.tile([P, TI, 2, 2 * TJ, 4], BF16, name="st", tag="st", bufs=2, align_bytes=64)
+                live[("st", m)] = rot.tile([P, TI, 2, TJ, 4], BF16, name="st", tag="st", bufs=2, align_bytes=64)
             dst = live[("st", m)][:, :, h]
             src = live[("h", n, 1)].rearrange("p t (i j) -> p i j t", i=TI)
             if n in SCALE_ON_VECTOR:
@@ -278,6 +276,13 @@ def tile_stateencoder_pa_kernel(
 
         def finish(o, r0, r1):
             zs = live[("zs", o)]
+            if o == NT - 1 and r1 == 4:
+                row0 = 512 * o + P * r0
+                for c in range(2):
+                    cols = slice(OUT // 2 * c, OUT // 2 * (c + 1))
+                    nc.scalar.activation(out=zs[:, r0, cols], in_=zs[:, r0, cols], func=ACT.Tanh)
+                    nc.sync.dma_start(out=out_rows[row0 : row0 + P, cols], in_=zs[:, r0, cols])
+                return
             flat = zs[:, r0:r1].rearrange("p r o -> p (r o)")
             nc.scalar.activation(out=flat, in_=flat, func=ACT.Tanh)
             for r in range(r0, r1):
@@ -290,9 +295,9 @@ def tile_stateencoder_pa_kernel(
 
         nc.gpsimd.tensor_tensor(out=dd, in0=mw[:, 0:1], in1=mw[:, 1:2], op=ALU.subtract)
         nc.gpsimd.tensor_scalar(out=dd, in0=dd, scalar1=30.0, scalar2=-30.0, op0=ALU.min, op1=ALU.max)
-        warm_ps = psum.tile([P, 512], F32, name="warm_ps", tag="z5", bufs=4)
 
         def warm_up(passes):
+            warm_ps = psum.tile([P, 512], F32, name="warm_ps", tag="pre", bufs=3)
             for step in range(passes):
                 nc.tensor.matmul(warm_ps, lhsT=warm[:, 0:P], rhs=warm, start=True, stop=True)
 
@@ -301,7 +306,7 @@ def tile_stateencoder_pa_kernel(
         x_transposes(1)
         x_codes(0, nc.vector.tensor_copy)
         copy_x4(0, 0, 1)
-        build_a(0, 2, 0, 1)
+        build_a(0, 1, 0, 1)
         quant_x4(0, 0, 1)
         build_b(0, 0, 1)
         regroup_w(0, 0, "V")
@@ -313,19 +318,19 @@ def tile_stateencoder_pa_kernel(
         quant_x4(0, 1, 2)
         btp = psum.tile([P, P], BF16, name="btp", tag="pre", bufs=3)
         nc.tensor.transpose(btp, bt, ident)
-        warm_up(4)
+        warm_up(6)
         nc.scalar.copy(out=bias_sb, in_=btp[:, 0:8])
         regroup_w(0, 2, "S")
         regroup_w(0, 3, "V")
         quant_w(0, 2)
         quant_w(0, 3)
-        build_a(2, 4, 0, 1)
+        build_a(1, 2, 0, 1)
         hidden(0, 0)
         nc.scalar.activation(out=rr, in_=dd, func=ACT.Exp)
         nc.gpsimd.tensor_scalar(out=den, in0=rr, scalar1=1.0, scalar2=0.0, op0=ALU.add, op1=ALU.add)
         regroup_w(1, 0, "V")
         copy_x4(1, 0, 2)
-        build_a(0, 2, 1, 2)
+        build_a(0, 1, 1, 2)
         quant_x4(1, 0, 2)
         quant_w(1, 0)
         build_b(0, 1, 2)
@@ -340,7 +345,7 @@ def tile_stateencoder_pa_kernel(
         nc.vector.reciprocal(out=w1, in_=den)
         nc.gpsimd.tensor_tensor(out=c1, in0=w1, in1=gm, op=ALU.mult)
         quant_w(1, 3)
-        build_a(2, 4, 1, 2)
+        build_a(1, 2, 1, 2)
         nc.vector.tensor_copy(
             out=w2g.rearrange("p (c i) k -> p c k i", i=4),
             in_=w2_raw.rearrange("p k (c i) -> p c k i", i=4),
@@ -353,6 +358,8 @@ def tile_stateencoder_pa_kernel(
                 hidden(n + 1, 1)
             if n == 3:
                 z_matmuls(0)
+            if n == NT:
+                warm_up(12)
             if 0 <= n - 1 < NT and n - 1 not in SCALE_ON_VECTOR:
                 scale_regroup(n - 1)
             if 0 <= n - 3 < NT:
@@ -376,8 +383,8 @@ def tile_stateencoder_pa_kernel(
             if n == 4:
                 copy_x4(3, 0, 2)
                 quant_x4(3, 0, 2)
-            if n == 3:
-                build_a(4, 8, 0, 2)
+            if n == 5:
+                build_a(2, 4, 0, 2)
             if n % 2 == 0 and 0 < n and n // 2 + 2 < NM:
                 build_b(n // 2 + 2, 0, 2)
             if 0 < n < NT:
@@ -403,6 +410,6 @@ def tile_stateencoder_pa_kernel(
             if n == NT + 1:
                 z_matmuls(NT - 1)
             if n - LAG >= 0:
-                pieces = 4 if n - LAG >= NT - 3 else 2
+                pieces = 4 if n - LAG >= NT - 3 else 2 if n - LAG >= 10 else 1
                 for piece in range(pieces):
                     finish(n - LAG, 4 * piece // pieces, 4 * (piece + 1) // pieces)

from contextlib import ExitStack

import concourse.mybir as mybir
from concourse.masks import make_identity

F32 = mybir.dt.float32
BF16 = mybir.dt.bfloat16
I32 = mybir.dt.int32
U32 = mybir.dt.uint32
U8 = mybir.dt.uint8
FP8X4 = mybir.dt.float8_e4m3fn_x4
ACT = mybir.ActivationFunctionType
ALU = mybir.AluOpType

P = 128
B, L, D, H, OUT = 2, 64, 512, 512, 640
TI, TJ = 16, 32
NT = B * L * L // 512
NM = NT // 2
FLOPS = 4 * 2 * (B * L) * D * H + 2 * (B * L * L) * H * OUT
SCALE_ON_VECTOR = (0, 1)
LAG = 3
X4_CHUNKS = ((0, 16), (16, 32), (32, 64), (64, 128))
TURN = 5
Z_FIRST = 3
Z_EARLY = 11
AHEAD = 3


def tile_stateencoder_pa_kernel(
    tc, global_outputs, sp_outputs, W_utt, b_utt, W_sp, b_sp, W2, b2, mix_w, gamma, out
):
    nc = tc.nc
    out_rows = out.rearrange("b i j o -> (b i j) o")
    with ExitStack() as ctx:
        keep = ctx.enter_context(tc.tile_pool(name="keep", bufs=1))
        rot = ctx.enter_context(tc.tile_pool(name="rot", bufs=2))
        psum = ctx.enter_context(tc.psum_pool(name="psum", bufs=1))
        ctx.enter_context(tc.manual_schedule())

        x_in = [global_outputs, sp_outputs]
        w_in = [W_utt, W_sp]
        x_sb = [keep.tile([P, D], BF16, name="x_sb%d" % s) for s in range(2)]
        w_raw = [keep.tile([P, 8, H], BF16, name="w_raw%d" % s) for s in range(2)]
        w2_raw = keep.tile([P, 4, OUT], BF16, name="w2_raw")
        bt = keep.tile([P, P], BF16, name="bt")
        b2b = keep.tile([P, OUT], BF16, name="b2b")
        mw = keep.tile([P, 2], BF16, name="mw")
        gm = keep.tile([P, 1], BF16, name="gm")
        ident = keep.tile([P, P], BF16, name="ident")
        zero1 = keep.tile([P, 1], F32, name="zero1")
        one1 = keep.tile([P, 1], F32, name="one1")

        nc.gpsimd.memset(bt, 0.0)
        nc.gpsimd.memset(zero1, 0.0)
        make_identity(nc, ident)
        with nc.allow_non_contiguous_dma(reason="small vectors"):
            nc.scalar.dma_start(out=mw, in_=mix_w.partition_broadcast(P))
            nc.scalar.dma_start(out=gm, in_=gamma.partition_broadcast(P))
        for s in range(2):
            nc.sync.dma_start(out=x_sb[s], in_=x_in[s].rearrange("b l d -> (b l) d"))
        for s in range(2):
            nc.sync.dma_start(out=bt[4 * s : 4 * s + 4, :], in_=[b_utt, b_sp][s].rearrange("(t p) -> t p", p=P))
        for s in range(2):
            w_view = w_in[s].rearrange("(s p) n -> p s n", p=P)
            pieces = 2 - s
            for piece in range(pieces):
                cols = slice(H * piece // pieces, H * (piece + 1) // pieces)
                nc.sync.dma_start(out=w_raw[s][:, :, cols], in_=w_view[:, :, cols])
        nc.sync.dma_start(out=w2_raw, in_=W2.rearrange("(k p) n -> p k n", p=P))
        nc.sync.dma_start(out=b2b, in_=b2.partition_broadcast(P))
        nc.scalar.activation(out=one1, in_=zero1, func=ACT.Exp)

        x1 = keep.tile([P, 2, P, 4], BF16, name="x1", align_bytes=64)
        xc1 = keep.tile([P, 2, P], U32, name="xc1", align_bytes=64)
        xs1 = keep.tile([P, 2, P], U8, name="xs1", align_bytes=64)
        xs4 = keep.tile([P, 8 * P], U8, name="xs4", align_bytes=64)
        a_c = keep.tile([P, 2, B * 2, 512], U32, name="a_c", align_bytes=64)
        a_s = keep.tile([P, 2, B * 2, 512], U8, name="a_s", align_bytes=64)
        wc = keep.tile([P, 2, 4, 256], U32, name="wc", align_bytes=64)
        ws = keep.tile([P, 2, 4, 256], U8, name="ws", align_bytes=64)
        w2g = keep.tile([P, OUT, 4], BF16, name="w2g", align_bytes=64)
        w2c = keep.tile([P, OUT], U32, name="w2c", align_bytes=64)
        w2s = keep.tile([P, OUT], U8, name="w2s", align_bytes=64)
        bias_sb = keep.tile([P, 8], F32, name="bias_sb")
        dd = keep.tile([P, 1], F32, name="dd")
        rr = keep.tile([P, 1], F32, name="rr")
        den = keep.tile([P, 1], F32, name="den")
        w1 = keep.tile([P, 1], F32, name="w1")
        c1 = keep.tile([P, 1], F32, name="c1")
        xs1_words = xs1.rearrange("p s c -> p (s c)").bitcast(I32).rearrange("p (s w) -> p s w", s=2)
        xs4_words = xs4.bitcast(I32)
        a_words = (
            a_s.rearrange("p s b c -> p (s b c)").bitcast(I32)
            .rearrange("p (s b i w) -> p s b i w", s=2, b=B * 2, i=TI)
        )

        warm = keep.tile([P, 512], BF16, name="warm")
        nc.vector.memset(warm, 0.0)
        nc.vector.memset(xs1.rearrange("p s c -> p (s c)").bitcast(I32), 0)
        nc.vector.memset(xs4_words, 0)

        live = {}
        w_grouped = {}

        def x_transposes(s):
            xt = psum.tile([P, 4, P], BF16, name="xt", tag="pre", bufs=3)
            for t in range(4):
                nc.tensor.transpose(xt[:, t, :], x_sb[s][:, P * t : P * (t + 1)], ident)
            live[("xt", s)] = xt

        def x_codes(s, copy):
            copy(out=x1[:, s], in_=live[("xt", s)].rearrange("p t r -> p r t"))
            nc.vector.quantize_mx(
                out=xc1[:, s, :].bitcast(FP8X4), scales=xs1[:, s, :],
                in_=x1[:, s].rearrange("p r t -> p (r t)"),
            )

        def copy_x4(chunk, s0, s1):
            tok0, tok1 = X4_CHUNKS[chunk]
            nt = tok1 - tok0
            if ("x4", chunk) not in live:
                live[("x4", chunk)] = rot.tile(
                    [P, 2, nt, 4, 4], BF16, name="x4_%d" % chunk, tag="x4_%d" % chunk, bufs=1, align_bytes=64
                )
            nc.vector.tensor_copy(
                out=live[("x4", chunk)][:, s0:s1],
                in_=x1[:, s0:s1, tok0:tok1, :].unsqueeze(3).to_broadcast([P, s1 - s0, nt, 4, 4]),
            )

        def quant_x4(chunk, s0, s1):
            tok0, tok1 = X4_CHUNKS[chunk]
            nt = 4 * (tok1 - tok0)
            xc4 = rot.tile([P, (s1 - s0) * nt], U32, name="xc4_%d" % chunk, tag="xc4_%d" % chunk, bufs=1, align_bytes=64)
            nc.vector.quantize_mx(
                out=xc4.bitcast(FP8X4), scales=xs4[:, 8 * tok0 + s0 * nt : 8 * tok0 + s1 * nt],
                in_=live[("x4", chunk)][:, s0:s1].rearrange("p s i c t -> p (s i c t)"),
            )

        def build_a(k0, k1, s0, s1):
            ns, nk = s1 - s0, k1 - k0
            nc.vector.tensor_copy(
                out=a_c[:, s0:s1, k0:k1, :].bitcast(I32).rearrange("p s k (i j) -> p s k i j", i=TI),
                in_=xc1[:, s0:s1, TJ * k0 : TJ * k1].bitcast(I32).rearrange("p s (k j) -> p s k j", j=TJ)
                .unsqueeze(3).to_broadcast([P, ns, nk, TI, TJ]),
            )
            nc.vector.tensor_copy(
                out=a_words[:, s0:s1, k0:k1],
                in_=xs1_words[:, s0:s1, TJ // 4 * k0 : TJ // 4 * k1].rearrange("p s (k w) -> p s k w", w=TJ // 4)
                .unsqueeze(3).to_broadcast([P, ns, nk, TI, TJ // 4]),
            )

        def build_b(m, s0, s1):
            if ("b", m) not in live:
                b_c = rot.tile([P, 2, 512], U32, name="b_c", tag="b_c", bufs=3, align_bytes=64)
                b_s = rot.tile([P, 2, 512], U8, name="b_s", tag="b_s", bufs=3, align_bytes=64)
                live[("b", m)] = (b_c, b_s)
            b_c, b_s = live[("b", m)]
            ns = s1 - s0
            nc.vector.tensor_copy(
                out=b_c[:, s0:s1].bitcast(I32).rearrange("p s (i j) -> p s i j", i=TI),
                in_=xc1[:, s0:s1, TI * m : TI * (m + 1)].bitcast(I32).unsqueeze(3).to_broadcast([P, ns, TI, TJ]),
            )
            tok0, tok1 = [c for c in X4_CHUNKS if c[0] <= TI * m < c[1]][0]
            words = xs4_words[:, 2 * tok0 : 2 * tok1].rearrange("p (s i) -> p s i", s=2)
            nc.vector.tensor_copy(
                out=b_s.rearrange("p s c -> p (s c)").bitcast(I32)
                .rearrange("p (s i w) -> p s i w", s=2, i=TI)[:, s0:s1],
                in_=words[:, s0:s1, TI * m - tok0 : TI * (m + 1) - tok0].unsqueeze(3)
                .to_broadcast([P, ns, TI, TJ // 4]),
            )

        def regroup_w(s, c, engine):
            wg = rot.tile([P, 2, P, 4], BF16, name="wg", tag="wg", bufs=4, align_bytes=64)
            src = w_raw[s][:, :, P * c : P * (c + 1)]
            if engine == "V":
                nc.vector.tensor_copy(
                    out=wg.rearrange("p g (c i) k -> p g c k i", i=4),
                    in_=src.rearrange("p (g k) (c i) -> p g c k i", g=2, i=4),
                )
            else:
                nc.scalar.copy(out=wg, in_=src.rearrange("p (g k) m -> p g m k", g=2))
            w_grouped[(s, c)] = wg

        def quant_w(s, c):
            nc.vector.quantize_mx(
                out=wc[:, s, c, :].bitcast(FP8X4), scales=ws[:, s, c, :],
                in_=w_grouped[(s, c)].rearrange("p g m k -> p (g m k)"),
            )

        def pre_act(n, s, t):
            m, h = divmod(n, 2)
            b = m // (NM // B)
            b_c, b_s = live[("b", m)]
            if ("h", n, s) not in live:
                live[("h", n, s)] = rot.tile([P, 4, 512], F32, name="hs%d" % s, tag="hs%d" % s, bufs=(AHEAD + 2, 3)[s])
            hs = live[("h", n, s)]
            pre = psum.tile([P, 512], F32, name="pre", tag="pre", bufs=3)
            k = 2 * b + h
            nc.tensor.matmul_mx(
                out=pre,
                lhsT=wc[:, s, t, 0:P].bitcast(FP8X4), lhsT_scale=ws[:, s, t, 0:P],
                rhs=a_c[:, s, k].bitcast(FP8X4), rhs_scale=a_s[:, s, k],
                start=True, stop=False,
            )
            nc.tensor.matmul_mx(
                out=pre,
                lhsT=wc[:, s, t, P : 2 * P].bitcast(FP8X4), lhsT_scale=ws[:, s, t, P : 2 * P],
                rhs=b_c[:, s].bitcast(FP8X4), rhs_scale=b_s[:, s],
                start=False, stop=True,
            )
            nc.scalar.activation(
                out=hs[:, t, :], in_=pre, func=ACT.Tanh,
                bias=bias_sb[:, 4 * s + t : 4 * s + t + 1], scale=1.0,
            )

        def mix(n):
            hu = live[("h", n, 0)].rearrange("p t w -> p (t w)")
            hp = live[("h", n, 1)].rearrange("p t w -> p (t w)")
            nc.vector.scalar_tensor_tensor(out=hp, in0=hu, scalar=rr[:, 0:1], in1=hp, op0=ALU.mult, op1=ALU.add)

        def scale_regroup(n):
            m, h = divmod(n, 2)
            if h == 0:
                live[("st", m)] = rot.tile([P, TI, 2, TJ, 4], BF16, name="st", tag="st", bufs=2, align_bytes=64)
            dst = live[("st", m)][:, :, h]
            src = live[("h", n, 1)].rearrange("p t (i j) -> p i j t", i=TI)
            if n in SCALE_ON_VECTOR:
                nc.vector.tensor_scalar(out=dst, in0=src, scalar1=c1[:, 0:1], scalar2=None, op0=ALU.mult)
            else:
                nc.gpsimd.tensor_scalar(out=dst, in0=src, scalar1=c1[:, 0:1], scalar2=0.0, op0=ALU.mult, op1=ALU.add)

        def quant_state(m, q0, q1):
            st = live[("st", m)][:, TI // 2 * q0 : TI // 2 * q1]
            cols = 512 * (q1 - q0)
            s_c = rot.tile([P, cols], U32, name="s_c%d" % (q1 - q0), tag="s_c%d" % (q1 - q0), bufs=2, align_bytes=64)
            s_s = rot.tile([P, cols], U8, name="s_s%d" % (q1 - q0), tag="s_s%d" % (q1 - q0), bufs=2, align_bytes=64)
            nc.vector.quantize_mx(out=s_c.bitcast(FP8X4), scales=s_s, in_=st.rearrange("p i h j t -> p (i h j t)"))
            for q in range(q0, q1):
                cols = slice(512 * (q - q0), 512 * (q - q0 + 1))
                live[("sc", 2 * m + q)] = (s_c[:, cols], s_s[:, cols])

        def z_matmuls(o):
            s_c, s_s = live[("sc", o)]
            z1 = psum.tile([P, 4, P], F32, name="z1", tag="z1", bufs=1)
            z5s = []
            for r in range(4):
                cols = slice(P * r, P * (r + 1))
                nc.tensor.matmul_mx(
                    out=z1[:, r, :], lhsT=s_c[:, cols].bitcast(FP8X4), lhsT_scale=s_s[:, cols],
                    rhs=w2c[:, 512:640].bitcast(FP8X4), rhs_scale=w2s[:, 512:640], start=True, stop=True,
                )
            for r in range(4):
                if o == NT - 2 and r < 3:
                    z5 = psum.tile([P, 512], F32, name="z5", tag="pre", bufs=3)
                else:
                    z5 = psum.tile([P, 512], F32, name="z5", tag="z5", bufs=4)
                z5s.append(z5)
                cols = slice(P * r, P * (r + 1))
                nc.tensor.matmul_mx(
                    out=z5, lhsT=s_c[:, cols].bitcast(FP8X4), lhsT_scale=s_s[:, cols],
                    rhs=w2c[:, 0:512].bitcast(FP8X4), rhs_scale=w2s[:, 0:512], start=True, stop=True,
                )
            live[("z", o)] = (z1, z5s)

        def add_b2(o):
            z1, z5s = live[("z", o)]
            zs = rot.tile([P, 4, OUT], F32, name="zs", tag="zs", bufs=3)
            live[("zs", o)] = zs
            nc.vector.tensor_tensor(
                out=zs[:, :, 512:640], in0=z1,
                in1=b2b[:, 512:640].unsqueeze(1).to_broadcast([P, 4, P]), op=ALU.add,
            )
            for r in range(4):
                nc.vector.tensor_tensor(out=zs[:, r, 0:512], in0=z5s[r], in1=b2b[:, 0:512], op=ALU.add)

        def finish(o, r0, r1):
            zs = live[("zs", o)]
            if o == NT - 1 and r1 == 4:
                row0 = 512 * o + P * r0
                for c in range(2):
                    cols = slice(OUT // 2 * c, OUT // 2 * (c + 1))
                    nc.scalar.activation(out=zs[:, r0, cols], in_=zs[:, r0, cols], func=ACT.Tanh)
                    nc.sync.dma_start(out=out_rows[row0 : row0 + P, cols], in_=zs[:, r0, cols])
                return
            flat = zs[:, r0:r1].rearrange("p r o -> p (r o)")
            nc.scalar.activation(out=flat, in_=flat, func=ACT.Tanh)
            for r in range(r0, r1):
                row0 = 512 * o + P * r
                nc.sync.dma_start(out=out_rows[row0 : row0 + P, :], in_=zs[:, r, :])

        def hidden(n, s):
            for t in range(4):
                pre_act(n, s, t)

        nc.gpsimd.tensor_tensor(out=dd, in0=mw[:, 0:1], in1=mw[:, 1:2], op=ALU.subtract)
        nc.gpsimd.tensor_scalar(out=dd, in0=dd, scalar1=30.0, scalar2=-30.0, op0=ALU.min, op1=ALU.max)

        def warm_up(passes):
            warm_ps = psum.tile([P, 512], F32, name="warm_ps", tag="pre", bufs=3)
            for step in range(passes):
                nc.tensor.matmul(warm_ps, lhsT=warm[:, 0:P], rhs=warm, start=True, stop=True)

        warm_up(4)
        x_transposes(0)
        x_transposes(1)
        x_codes(0, nc.vector.tensor_copy)
        copy_x4(0, 0, 1)
        build_a(0, 1, 0, 1)
        quant_x4(0, 0, 1)
        build_b(0, 0, 1)
        regroup_w(0, 0, "V")
        x_codes(1, nc.scalar.copy)
        regroup_w(0, 1, "S")
        quant_w(0, 0)
        copy_x4(0, 1, 2)
        quant_w(0, 1)
        quant_x4(0, 1, 2)
        btp = psum.tile([P, P], BF16, name="btp", tag="pre", bufs=3)
        nc.tensor.transpose(btp, bt, ident)
        warm_up(6)
        nc.scalar.copy(out=bias_sb, in_=btp[:, 0:8])
        regroup_w(0, 2, "S")
        regroup_w(0, 3, "V")
        quant_w(0, 2)
        quant_w(0, 3)
        build_a(1, 2, 0, 1)
        hidden(0, 0)
        nc.scalar.activation(out=rr, in_=dd, func=ACT.Exp)
        nc.gpsimd.tensor_scalar(out=den, in0=rr, scalar1=1.0, scalar2=0.0, op0=ALU.add, op1=ALU.add)
        regroup_w(1, 0, "V")
        copy_x4(1, 0, 2)
        build_a(0, 1, 1, 2)
        quant_x4(1, 0, 2)
        quant_w(1, 0)
        build_b(0, 1, 2)
        build_b(1, 0, 2)
        regroup_w(1, 1, "V")
        hidden(1, 0)
        regroup_w(1, 2, "V")
        hidden(2, 0)
        quant_w(1, 1)
        regroup_w(1, 3, "V")
        quant_w(1, 2)
        nc.vector.reciprocal(out=w1, in_=den)
        nc.gpsimd.tensor_tensor(out=c1, in0=w1, in1=gm, op=ALU.mult)
        quant_w(1, 3)
        build_a(1, 2, 1, 2)
        nc.vector.tensor_copy(
            out=w2g.rearrange("p (c i) k -> p c k i", i=4),
            in_=w2_raw.rearrange("p k (c i) -> p c k i", i=4),
        )

        for n in range(NT + LAG):
            if n <= TURN:
                hidden(n, 1)
            if n == TURN:
                hidden(n + 1, 1)
            if n == 3:
                z_matmuls(0)
            if n == NT:
                warm_up(12)
            if 0 <= n - 1 < NT and n - 1 not in SCALE_ON_VECTOR:
                scale_regroup(n - 1)
            if 0 <= n - 3 < NT:
                add_b2(n - 3)
            if n == NT:
                quant_state(NM - 1, 0, 1)
                quant_state(NM - 1, 1, 2)
            if n % 2 == 0 and 2 <= n < NT:
                quant_state(n // 2 - 1, 0, 2)
            if n == 0:
                copy_x4(2, 0, 2)
                mix(0)
                quant_x4(2, 0, 2)
                build_b(2, 0, 2)
                flat = w2g.rearrange("p n k -> p (n k)")
                scale_regroup(0)
                nc.vector.quantize_mx(out=w2c[:, 0:512].bitcast(FP8X4), scales=w2s[:, 0:512], in_=flat[:, 0:2048])
                nc.vector.quantize_mx(
                    out=w2c[:, 512:640].bitcast(FP8X4), scales=w2s[:, 512:640], in_=flat[:, 2048:2560]
                )
            if n == 4:
                copy_x4(3, 0, 2)
                quant_x4(3, 0, 2)
            if n == 5:
                build_a(2, 4, 0, 2)
            if n % 2 == 0 and 0 < n and n // 2 + 2 < NM:
                build_b(n // 2 + 2, 0, 2)
            if 0 < n < NT:
                mix(n)
                if n in SCALE_ON_VECTOR:
                    scale_regroup(n)
            if n < TURN:
                hidden(n + AHEAD, 0)
            if n <= TURN:
                if n > 2:
                    z_matmuls(n - 2)
            else:
                ahead = [(n + 1, 1, t) for t in range(4)] if n + 1 < NT else []
                if n + AHEAD - 1 < NT:
                    ahead = ahead + [(n + AHEAD - 1, 0, t) for t in range(4)]
                pos = min(len(ahead), Z_FIRST if n >= Z_EARLY else 8)
                for args in ahead[:pos]:
                    pre_act(args[0], args[1], args[2])
                if n - 2 < NT - 1:
                    z_matmuls(n - 2)
                for args in ahead[pos:]:
                    pre_act(args[0], args[1], args[2])
            if n == NT + 1:
                z_matmuls(NT - 1)
            if n - LAG >= 0:
                pieces = 4 if n - LAG >= NT - 3 else 2 if n - LAG >= 10 else 1
                for piece in range(pieces):
                    finish(n - LAG, 4 * piece // pieces, 4 * (piece + 1) // pieces)
